import numpy as np
import ml_dtypes


def mxq(x, axis, fmt="e4m3"):
    dtype, down = {"e4m3": (ml_dtypes.float8_e4m3fn, 7), "e5m2": (ml_dtypes.float8_e5m2, 14)}[fmt]
    v = np.moveaxis(np.asarray(x, np.float32).astype(ml_dtypes.bfloat16).astype(np.float64), axis, -1)
    blocks = v.reshape(v.shape[:-1] + (-1, 32))
    amax = np.abs(blocks).max(-1, keepdims=True)
    byte = np.maximum(np.where(amax > 0, np.frexp(amax)[1] - 1 + 127, 0) - down, 1)
    scale = np.exp2(byte - 127.0)
    codes = (blocks / scale).astype(np.float32).astype(dtype).astype(np.float64)
    return np.moveaxis((codes * scale).reshape(v.shape), -1, axis)


WIDE = False


def mx_kscale(k):
    if not WIDE:
        return np.ones(k)
    levels = np.array([10, -10, 5, -5, 0])
    a = np.random.permutation(np.resize(levels, k // 512 * 4)).reshape(k // 512, 4)
    idx = np.arange(k)
    return np.exp2(a[idx // 512, idx % 128 // 32])


BF16 = ml_dtypes.bfloat16


def bf(x):
    return np.asarray(x, np.float32).astype(BF16)


def f64(x):
    return np.asarray(x).astype(np.float64)


E2M1 = np.array([0.0, 0.5, 1.0, 1.5, 2.0, 3.0, 4.0, 6.0, -0.0, -0.5, -1.0, -1.5, -2.0, -3.0, -4.0, -6.0])


def pack_weight(w, fmt):
    k, n = w.shape
    w = f64(bf(w)).reshape(k // 32, 32, n)
    amax = np.abs(w).max(1)
    if fmt == "e4m3":
        byte = np.frexp(amax)[1] - 1 + 127 - 7
    else:
        mant, ex = np.frexp(amax / 6.0)
        byte = np.where(mant > 0.5, ex, ex - 1) + 127
    byte = np.clip(np.where(amax > 0, byte, 1), 1, 254)
    scaled = (w * np.exp2(127.0 - byte)[:, None, :]).reshape(k, n).astype(np.float32)
    by_word = np.ascontiguousarray(scaled.reshape(k // 512, 128, 4, n).transpose(0, 1, 3, 2))
    if fmt == "e4m3":
        words = by_word.astype(ml_dtypes.float8_e4m3fn).view(np.uint8)
    else:
        c = by_word.astype(ml_dtypes.float4_e2m1fn).view(np.uint8) & 0xF
        words = c[..., 0::2] | (c[..., 1::2] << 4)
    return np.ascontiguousarray(words), np.ascontiguousarray(byte.astype(np.uint8).reshape(k // 512, 16, n))


def unpack_weight(words, scales, fmt):
    g, p, n, _ = words.shape
    if fmt == "e4m3":
        vals = np.ascontiguousarray(words).view(ml_dtypes.float8_e4m3fn).astype(np.float64)
    else:
        nib = np.empty((g, p, n, 4), np.uint8)
        nib[..., 0::2] = words & 0xF
        nib[..., 1::2] = words >> 4
        vals = E2M1[nib]
    vals = vals * np.repeat(np.exp2(scales.astype(np.float64) - 127.0), 8, axis=1)[..., None]
    return vals.transpose(0, 1, 3, 2).reshape(g * 512, n)


B, S, E, H, D = 1, 512, 2048, 16, 128
ROPE_BASE = 10000.0
HALF = D // 2
FMT = "e4m3"


def rope_interleaved(t):
    inv_freq = 1.0 / (ROPE_BASE ** (np.arange(HALF) * 2.0 / D))
    ang = np.arange(S)[:, None] * inv_freq[None, :]
    cos = np.cos(ang)[None, :, None, :]
    sin = np.sin(ang)[None, :, None, :]
    t0 = t[..., 0::2]
    t1 = t[..., 1::2]
    out = np.stack([t0 * cos - t1 * sin, t1 * cos + t0 * sin], axis=-1)
    return out.reshape(B, S, H, D)


def setup_inputs():
    s = mx_kscale(E)
    x = bf(np.random.standard_normal((B, S, E)) * s)
    Wq_words, Wq_scales = pack_weight(np.random.standard_normal((E, H * D)) / np.sqrt(E) / s[:, None], FMT)
    Wk_words, Wk_scales = pack_weight(np.random.standard_normal((E, H * D)) / np.sqrt(E) / s[:, None], FMT)
    return {"x": x,
            "Wq_words": Wq_words, "Wq_scales": Wq_scales,
            "Wk_words": Wk_words, "Wk_scales": Wk_scales}


def reference(x, Wq_words, Wq_scales, Wk_words, Wk_scales):
    xq = mxq(f64(x), 2, "e4m3")
    q = (xq @ unpack_weight(Wq_words, Wq_scales, FMT)).reshape(B, S, H, D)
    k = (xq @ unpack_weight(Wk_words, Wk_scales, FMT)).reshape(B, S, H, D)
    q = rope_interleaved(q)
    k = rope_interleaved(k)
    return q.transpose(0, 2, 1, 3), k.transpose(0, 2, 1, 3)

@@ -1,0 +1,227 @@
+import math
+
+import concourse.mybir as mybir
+from concourse.masks import make_identity
+
+F32 = mybir.dt.float32
+BF16 = mybir.dt.bfloat16
+I32 = mybir.dt.int32
+U32 = mybir.dt.uint32
+U8 = mybir.dt.uint8
+FP8X4 = mybir.dt.float8_e4m3fn_x4
+ALU = mybir.AluOpType
+ACT = mybir.ActivationFunctionType
+
+P = 128
+SEQ = 512
+EMB = 2048
+HEADS = 16
+HEAD_DIM = 128
+HALF = HEAD_DIM // 2
+HALF_LOG2 = 6
+assert 2**HALF_LOG2 == HALF
+ROPE_BASE = 10000.0
+
+PACK = 4
+K_PASS = P * PACK
+PASSES = EMB // K_PASS
+POS_TILES = SEQ // P
+N_TILE = 512
+TILE_HEADS = N_TILE // HEAD_DIM
+COL_TILES = HEADS * HEAD_DIM // N_TILE
+PLANE_ROWS = 4
+QUADRANTS = 4
+
+TWO_PI = 2.0 * math.pi
+TWO_PI_HEAD = int(TWO_PI * 2.0**14) / 2.0**14
+TWO_PI_TAIL = TWO_PI - TWO_PI_HEAD
+ROUND_MAGIC = 1.5 * 2.0**23
+
+FLOPS = 2 * SEQ * EMB * 2 * HEADS * HEAD_DIM
+
+
+def build_rotation_table(nc, pool):
+    zero = pool.tile([P, 1], F32, name="zero")
+    warm = pool.tile([P, 1], F32, name="warm")
+    nc.vector.memset(zero[:], 0.0)
+    nc.scalar.activation(out=warm[:], in_=zero[:], func=ACT.Sin)
+
+    freq = pool.tile([P, HALF], F32, name="freq")
+    nc.vector.memset(freq[:, 0:1], 1.0)
+    for step in range(HALF_LOG2):
+        width = 2**step
+        nc.vector.tensor_scalar_mul(
+            out=freq[:, width : 2 * width],
+            in0=freq[:, 0:width],
+            scalar1=ROPE_BASE ** (-2.0 * width / HEAD_DIM),
+        )
+
+    position_int = pool.tile([P, POS_TILES], I32, name="position_int")
+    nc.gpsimd.iota(position_int[:], pattern=[[1, POS_TILES]], base=0, channel_multiplier=POS_TILES)
+    position = pool.tile([P, POS_TILES], F32, name="position")
+    nc.vector.tensor_copy(out=position[:], in_=position_int[:])
+
+    shape = [P, POS_TILES, HALF]
+    angle = pool.tile(shape, F32, name="angle")
+    nc.vector.tensor_tensor(
+        out=angle[:],
+        in0=position[:].unsqueeze(2).to_broadcast(shape),
+        in1=freq[:].unsqueeze(1).to_broadcast(shape),
+        op=ALU.mult,
+    )
+
+    shifted = pool.tile(shape, F32, name="shifted")
+    turns = pool.tile(shape, F32, name="turns")
+    coarse = pool.tile(shape, F32, name="coarse")
+    reduced = pool.tile(shape, F32, name="reduced")
+    nc.vector.tensor_scalar(
+        out=shifted[:], in0=angle[:], scalar1=1.0 / TWO_PI, scalar2=ROUND_MAGIC, op0=ALU.mult, op1=ALU.add
+    )
+    nc.vector.tensor_scalar_sub(out=turns[:], in0=shifted[:], scalar1=ROUND_MAGIC)
+    nc.vector.scalar_tensor_tensor(
+        out=coarse[:], in0=turns[:], scalar=-TWO_PI_HEAD, in1=angle[:], op0=ALU.mult, op1=ALU.add
+    )
+    nc.vector.scalar_tensor_tensor(
+        out=reduced[:], in0=turns[:], scalar=-TWO_PI_TAIL, in1=coarse[:], op0=ALU.mult, op1=ALU.add
+    )
+
+    sin_half = pool.tile(shape, F32, name="sin_half")
+    sin_quarter = pool.tile(shape, F32, name="sin_quarter")
+    nc.scalar.activation(out=sin_half[:], in_=reduced[:], func=ACT.Sin, scale=0.5)
+    nc.scalar.activation(out=sin_quarter[:], in_=reduced[:], func=ACT.Sin, scale=0.25)
+
+    cos_half_less_1 = pool.tile(shape, F32, name="cos_half_less_1")
+    half_sin = pool.tile(shape, F32, name="half_sin")
+    cos_less_1 = pool.tile(shape, F32, name="cos_less_1")
+    nc.vector.scalar_tensor_tensor(
+        out=cos_half_less_1[:], in0=sin_quarter[:], scalar=-2.0, in1=sin_quarter[:], op0=ALU.mult, op1=ALU.mult
+    )
+    nc.vector.scalar_tensor_tensor(
+        out=cos_less_1[:], in0=sin_half[:], scalar=-2.0, in1=sin_half[:], op0=ALU.mult, op1=ALU.mult
+    )
+    nc.vector.scalar_tensor_tensor(
+        out=half_sin[:], in0=cos_half_less_1[:], scalar=1.0, in1=sin_half[:], op0=ALU.add, op1=ALU.mult
+    )
+
+    table = pool.tile([P, POS_TILES, 2, HALF, 2], F32, name="table")
+    nc.vector.tensor_scalar_add(out=table[:, :, 0, :, 0], in0=cos_less_1[:], scalar1=1.0)
+    nc.vector.tensor_scalar_add(out=table[:, :, 1, :, 1], in0=cos_less_1[:], scalar1=1.0)
+    nc.vector.tensor_scalar_mul(out=table[:, :, 0, :, 1], in0=half_sin[:], scalar1=2.0)
+    nc.vector.tensor_scalar_mul(out=table[:, :, 1, :, 0], in0=half_sin[:], scalar1=-2.0)
+    return table
+
+
+def load_scale_planes(nc, planes, scales):
+    for quadrant in range(QUADRANTS):
+        first = 32 * quadrant
+        nc.sync.dma_start(
+            out=planes[first : first + PASSES * PLANE_ROWS, :].bitcast(I32),
+            in_=scales[:, PLANE_ROWS * quadrant : PLANE_ROWS * (quadrant + 1), :].bitcast(I32),
+        )
+
+
+def load_weight_columns(nc, words_tile, words, col_tile):
+    columns = slice(col_tile * N_TILE, (col_tile + 1) * N_TILE)
+    nc.sync.dma_start(
+        out=words_tile[:].bitcast(I32),
+        in_=words[:, :, columns, :].rearrange("g p n t -> p g (n t)").bitcast(I32),
+    )
+
+
+def tile_multiheadselfattention_pa_kernel(
+    tc, x, Wq_words, Wq_scales, Wk_words, Wk_scales, out_0, out_1
+):
+    nc = tc.nc
+    weights = [(Wq_words, Wq_scales, out_0), (Wk_words, Wk_scales, out_1)]
+
+    with tc.manual_schedule(), tc.tile_pool(name="keep", bufs=1) as keep, tc.tile_pool(
+        name="products", bufs=4
+    ) as products, tc.tile_pool(name="results", bufs=3) as results, tc.psum_pool(name="psum", bufs=8) as psum:
+        x_rows = x.rearrange("b (m j) k -> m (b j) k", j=POS_TILES)
+        x_tiles = []
+        for j in range(POS_TILES):
+            x_tile = keep.tile([P, EMB], BF16, name="x%d" % j)
+            nc.sync.dma_start(out=x_tile[:], in_=x_rows[:, j, :])
+            x_tiles.append(x_tile)
+
+        plane_tiles = []
+        for w in range(len(weights)):
+            planes = keep.tile([P, HEADS * HEAD_DIM], U8, name="planes%d" % w, align_bytes=64)
+            nc.vector.memset(planes[:].bitcast(I32), 0)
+            plane_tiles.append(planes)
+
+        word_tiles = []
+        for w, (words, scales, out) in enumerate(weights):
+            load_scale_planes(nc, plane_tiles[w], scales)
+            for col_tile in range(COL_TILES):
+                words_tile = keep.tile([P, PASSES, N_TILE], U32, name="w%d_%d" % (w, col_tile), align_bytes=64)
+                load_weight_columns(nc, words_tile, words, col_tile)
+                word_tiles.append(words_tile)
+
+        identity = keep.tile([P, P], F32, name="identity")
+        make_identity(nc, identity[:])
+        table = build_rotation_table(nc, keep)
+
+        x_codes = []
+        x_planes = []
+        for j in range(POS_TILES):
+            pair_words = x_tiles[j][:].bitcast(F32)
+            grouped = keep.tile([P, PASSES * P * PACK], BF16, name="grouped%d" % j, align_bytes=64)
+            grouped_words = grouped[:].bitcast(F32).rearrange("p (g m u) -> p g m u", g=PASSES, u=2)
+            for first_pass in range(0, PASSES, 2):
+                flipped = psum.tile([P, 2, 2, P], F32, name="flipped", tag="bank")
+                for g in range(first_pass, first_pass + 2):
+                    for u in range(2):
+                        nc.tensor.transpose(
+                            out=flipped[:, g - first_pass, u, :],
+                            in_=pair_words[:, 2 * P * g + u : 2 * P * (g + 1) : 2],
+                            identity=identity[:],
+                        )
+                nc.scalar.copy(
+                    out=grouped_words[:, first_pass : first_pass + 2, :, :],
+                    in_=flipped[:].rearrange("p g u m -> p g m u"),
+                )
+            codes = keep.tile([P, PASSES * P], U32, name="x_codes%d" % j, align_bytes=64)
+            plane = keep.tile([P, PASSES * P], U8, name="x_plane%d" % j, align_bytes=64)
+            nc.vector.quantize_mx(out=codes[:].bitcast(FP8X4), scales=plane[:], in_=grouped[:])
+            x_codes.append(codes)
+            x_planes.append(plane)
+
+        pair_shape = [P, 2, TILE_HEADS, HALF, 2]
+        for w, (words, scales, out) in enumerate(weights):
+            out_rows = out.rearrange("b h (m j) d -> m (b h) (j d)", j=POS_TILES)
+            for col_tile in range(COL_TILES):
+                words_tile = word_tiles[w * COL_TILES + col_tile]
+                columns = slice(col_tile * N_TILE, (col_tile + 1) * N_TILE)
+                rotated = results.tile([P, TILE_HEADS, POS_TILES, HEAD_DIM], F32, name="rotated")
+                for j in range(POS_TILES):
+                    sums = psum.tile([P, N_TILE], F32, name="sums", tag="bank")
+                    for g in range(PASSES):
+                        positions = slice(g * P, (g + 1) * P)
+                        nc.tensor.matmul_mx(
+                            out=sums[:],
+                            lhsT=x_codes[j][:, positions].bitcast(FP8X4),
+                            lhsT_scale=x_planes[j][:, positions],
+                            rhs=words_tile[:, g, :].bitcast(FP8X4),
+                            rhs_scale=plane_tiles[w][PLANE_ROWS * g : P, columns],
+                            start=(g == 0),
+                            stop=(g == PASSES - 1),
+                        )
+                    terms = products.tile(pair_shape, F32, name="terms")
+                    nc.vector.tensor_tensor(
+                        out=terms[:],
+                        in0=sums[:]
+                        .rearrange("p (h i v) -> p v h i", h=TILE_HEADS, v=2)
+                        .unsqueeze(4)
+                        .to_broadcast(pair_shape),
+                        in1=table[:, j].unsqueeze(2).to_broadcast(pair_shape),
+                        op=ALU.mult,
+                    )
+                    nc.gpsimd.tensor_tensor(
+                        out=rotated[:, :, j, :],
+                        in0=terms[:, 0].rearrange("p h i e -> p h (i e)"),
+                        in1=terms[:, 1].rearrange("p h i e -> p h (i e)"),
+                        op=ALU.add,
+                    )
+                heads = slice(col_tile * TILE_HEADS, (col_tile + 1) * TILE_HEADS)
+                nc.scalar.dma_start(out=out_rows[:, heads, :], in_=rotated[:].rearrange("m h j d -> m h (j d)"))

@@ -135,7 +135,7 @@ def tile_multiheadselfattention_pa_kernel(
     weights = [(Wq_words, Wq_scales, out_0), (Wk_words, Wk_scales, out_1)]
 
     with tc.manual_schedule(), tc.tile_pool(name="keep", bufs=1) as keep, tc.tile_pool(
-        name="products", bufs=4
+        name="products", bufs=3
     ) as products, tc.tile_pool(name="results", bufs=3) as results, tc.psum_pool(name="psum", bufs=8) as psum:
         x_rows = x.rearrange("b (m j) k -> m (b j) k", j=POS_TILES)
         x_tiles = []
@@ -194,6 +194,7 @@ def tile_multiheadselfattention_pa_kernel(
                 words_tile = word_tiles[w * COL_TILES + col_tile]
                 columns = slice(col_tile * N_TILE, (col_tile + 1) * N_TILE)
                 rotated = results.tile([P, TILE_HEADS, POS_TILES, HEAD_DIM], F32, name="rotated")
+                terms = products.tile([P, POS_TILES] + pair_shape[1:], F32, name="terms")
                 for j in range(POS_TILES):
                     sums = psum.tile([P, N_TILE], F32, name="sums", tag="bank")
                     for g in range(PASSES):
@@ -207,9 +208,8 @@ def tile_multiheadselfattention_pa_kernel(
                             start=(g == 0),
                             stop=(g == PASSES - 1),
                         )
-                    terms = products.tile(pair_shape, F32, name="terms")
                     nc.vector.tensor_tensor(
-                        out=terms[:],
+                        out=terms[:, j],
                         in0=sums[:]
                         .rearrange("p (h i v) -> p v h i", h=TILE_HEADS, v=2)
                         .unsqueeze(4)
@@ -217,11 +217,23 @@ def tile_multiheadselfattention_pa_kernel(
                         in1=table[:, j].unsqueeze(2).to_broadcast(pair_shape),
                         op=ALU.mult,
                     )
+                heads = slice(col_tile * TILE_HEADS, (col_tile + 1) * TILE_HEADS)
+                if w == len(weights) - 1 and col_tile == COL_TILES - 1:
+                    for j in range(POS_TILES):
+                        nc.vector.tensor_tensor(
+                            out=rotated[:, :, j, :],
+                            in0=terms[:, j, 0].rearrange("p h i e -> p h (i e)"),
+                            in1=terms[:, j, 1].rearrange("p h i e -> p h (i e)"),
+                            op=ALU.add,
+                        )
+                        nc.sync.dma_start(
+                            out=out_rows[:, heads, j * HEAD_DIM : (j + 1) * HEAD_DIM], in_=rotated[:, :, j, :]
+                        )
+                else:
                     nc.gpsimd.tensor_tensor(
-                        out=rotated[:, :, j, :],
-                        in0=terms[:, 0].rearrange("p h i e -> p h (i e)"),
-                        in1=terms[:, 1].rearrange("p h i e -> p h (i e)"),
+                        out=rotated[:].rearrange("p h j d -> p j h d"),
+                        in0=terms[:, :, 0].rearrange("p j h i e -> p j h (i e)"),
+                        in1=terms[:, :, 1].rearrange("p j h i e -> p j h (i e)"),
                         op=ALU.add,
                     )
-                heads = slice(col_tile * TILE_HEADS, (col_tile + 1) * TILE_HEADS)
-                nc.scalar.dma_start(out=out_rows[:, heads, :], in_=rotated[:].rearrange("m h j d -> m h (j d)"))
+                    nc.scalar.dma_start(out=out_rows[:, heads, :], in_=rotated[:].rearrange("m h j d -> m h (j d)"))

@@ -18,8 +18,9 @@ EMB = 2048
 HEADS = 16
 HEAD_DIM = 128
 HALF = HEAD_DIM // 2
-HALF_LOG2 = 6
-assert 2**HALF_LOG2 == HALF
+RADIX = 4
+DIGITS = 3
+assert RADIX**DIGITS == HALF
 ROPE_BASE = 10000.0
 
 PACK = 4
@@ -40,33 +41,44 @@ ROUND_MAGIC = 1.5 * 2.0**23
 FLOPS = 2 * SEQ * EMB * 2 * HEADS * HEAD_DIM
 
 
-def build_rotation_table(nc, pool):
-    zero = pool.tile([P, 1], F32, name="zero")
-    warm = pool.tile([P, 1], F32, name="warm")
-    nc.vector.memset(zero[:], 0.0)
-    nc.scalar.activation(out=warm[:], in_=zero[:], func=ACT.Sin)
-
-    freq = pool.tile([P, HALF], F32, name="freq")
-    nc.vector.memset(freq[:, 0:1], 1.0)
-    for step in range(HALF_LOG2):
-        width = 2**step
-        nc.vector.tensor_scalar_mul(
-            out=freq[:, width : 2 * width],
-            in0=freq[:, 0:width],
-            scalar1=ROPE_BASE ** (-2.0 * width / HEAD_DIM),
-        )
-
+def build_reduced_angles(nc, pool):
     position_int = pool.tile([P, POS_TILES], I32, name="position_int")
     nc.gpsimd.iota(position_int[:], pattern=[[1, POS_TILES]], base=0, channel_multiplier=POS_TILES)
+
+    powers = pool.tile([P, DIGITS, RADIX], F32, name="powers")
+    nc.vector.memset(powers[:], 1.0)
+    for digit in range(DIGITS):
+        for c in range(1, RADIX):
+            nc.vector.tensor_scalar_mul(
+                out=powers[:, digit, c : c + 1],
+                in0=powers[:, digit, 0:1],
+                scalar1=ROPE_BASE ** (-2.0 * c * RADIX**digit / HEAD_DIM),
+            )
     position = pool.tile([P, POS_TILES], F32, name="position")
     nc.vector.tensor_copy(out=position[:], in_=position_int[:])
 
+    square = [P, RADIX, RADIX]
+    low = pool.tile(square, F32, name="low")
+    nc.vector.tensor_tensor(
+        out=low[:],
+        in0=powers[:, 1, :].unsqueeze(2).to_broadcast(square),
+        in1=powers[:, 0, :].unsqueeze(1).to_broadcast(square),
+        op=ALU.mult,
+    )
+    high = pool.tile([P, POS_TILES, RADIX], F32, name="high")
+    nc.vector.tensor_tensor(
+        out=high[:],
+        in0=position[:].unsqueeze(2).to_broadcast([P, POS_TILES, RADIX]),
+        in1=powers[:, 2, :].unsqueeze(1).to_broadcast([P, POS_TILES, RADIX]),
+        op=ALU.mult,
+    )
     shape = [P, POS_TILES, HALF]
+    outer = [P, POS_TILES * RADIX, RADIX * RADIX]
     angle = pool.tile(shape, F32, name="angle")
     nc.vector.tensor_tensor(
-        out=angle[:],
-        in0=position[:].unsqueeze(2).to_broadcast(shape),
-        in1=freq[:].unsqueeze(1).to_broadcast(shape),
+        out=angle[:].rearrange("p j (a f) -> p (j a) f", a=RADIX),
+        in0=high[:].rearrange("p j a -> p (j a)").unsqueeze(2).to_broadcast(outer),
+        in1=low[:].rearrange("p b c -> p (b c)").unsqueeze(1).to_broadcast(outer),
         op=ALU.mult,
     )
 
@@ -84,15 +96,20 @@ def build_rotation_table(nc, pool):
     nc.vector.scalar_tensor_tensor(
         out=reduced[:], in0=turns[:], scalar=-TWO_PI_TAIL, in1=coarse[:], op0=ALU.mult, op1=ALU.add
     )
+    return reduced
 
+
+def build_rotation_table(nc, pool, reduced):
+    shape = [P, POS_TILES, HALF]
     sin_half = pool.tile(shape, F32, name="sin_half")
     sin_quarter = pool.tile(shape, F32, name="sin_quarter")
-    nc.scalar.activation(out=sin_half[:], in_=reduced[:], func=ACT.Sin, scale=0.5)
     nc.scalar.activation(out=sin_quarter[:], in_=reduced[:], func=ACT.Sin, scale=0.25)
+    nc.scalar.activation(out=sin_half[:], in_=reduced[:], func=ACT.Sin, scale=0.5)
 
     cos_half_less_1 = pool.tile(shape, F32, name="cos_half_less_1")
     half_sin = pool.tile(shape, F32, name="half_sin")
     cos_less_1 = pool.tile(shape, F32, name="cos_less_1")
+    table = pool.tile([P, POS_TILES, 2, HALF, 2], F32, name="table")
     nc.vector.scalar_tensor_tensor(
         out=cos_half_less_1[:], in0=sin_quarter[:], scalar=-2.0, in1=sin_quarter[:], op0=ALU.mult, op1=ALU.mult
     )
@@ -102,8 +119,6 @@ def build_rotation_table(nc, pool):
     nc.vector.scalar_tensor_tensor(
         out=half_sin[:], in0=cos_half_less_1[:], scalar=1.0, in1=sin_half[:], op0=ALU.add, op1=ALU.mult
     )
-
-    table = pool.tile([P, POS_TILES, 2, HALF, 2], F32, name="table")
     nc.vector.tensor_scalar_add(out=table[:, :, 0, :, 0], in0=cos_less_1[:], scalar1=1.0)
     nc.vector.tensor_scalar_add(out=table[:, :, 1, :, 1], in0=cos_less_1[:], scalar1=1.0)
     nc.vector.tensor_scalar_mul(out=table[:, :, 0, :, 1], in0=half_sin[:], scalar1=2.0)
@@ -120,12 +135,17 @@ def load_scale_planes(nc, planes, scales):
         )
 
 
-def load_weight_columns(nc, words_tile, words, col_tile):
-    columns = slice(col_tile * N_TILE, (col_tile + 1) * N_TILE)
+def load_weight_columns(nc, words_tile, words, first, width):
     nc.sync.dma_start(
         out=words_tile[:].bitcast(I32),
-        in_=words[:, :, columns, :].rearrange("g p n t -> p g (n t)").bitcast(I32),
+        in_=words[:, :, first : first + width, :].rearrange("g p n t -> p g (n t)").bitcast(I32),
     )
+
+
+def column_pieces(w, col_tile):
+    if w == 0 and col_tile == 0:
+        return [N_TILE // 2, N_TILE // 2]
+    return [N_TILE]
 
 
 def tile_multiheadselfattention_pa_kernel(
@@ -144,6 +164,14 @@ def tile_multiheadselfattention_pa_kernel(
             nc.sync.dma_start(out=x_tile[:], in_=x_rows[:, j, :])
             x_tiles.append(x_tile)
 
+        zero = keep.tile([P, 1], F32, name="zero")
+        warm = keep.tile([P, 1], F32, name="warm")
+        nc.vector.memset(zero[:], 0.0)
+        nc.scalar.activation(out=warm[:], in_=zero[:], func=ACT.Sin)
+        reduced = build_reduced_angles(nc, keep)
+        identity = keep.tile([P, P], F32, name="identity")
+        make_identity(nc, identity[:])
+
         plane_tiles = []
         for w in range(len(weights)):
             planes = keep.tile([P, HEADS * HEAD_DIM], U8, name="planes%d" % w, align_bytes=64)
@@ -154,13 +182,18 @@ def tile_multiheadselfattention_pa_kernel(
         for w, (words, scales, out) in enumerate(weights):
             load_scale_planes(nc, plane_tiles[w], scales)
             for col_tile in range(COL_TILES):
-                words_tile = keep.tile([P, PASSES, N_TILE], U32, name="w%d_%d" % (w, col_tile), align_bytes=64)
-                load_weight_columns(nc, words_tile, words, col_tile)
-                word_tiles.append(words_tile)
+                piece_tiles = []
+                offset = 0
+                for width in column_pieces(w, col_tile):
+                    words_tile = keep.tile(
+                        [P, PASSES, width], U32, name="w%d_%d_%d" % (w, col_tile, offset), align_bytes=64
+                    )
+                    load_weight_columns(nc, words_tile, words, col_tile * N_TILE + offset, width)
+                    piece_tiles.append((words_tile, offset, width))
+                    offset += width
+                word_tiles.append(piece_tiles)
 
-        identity = keep.tile([P, P], F32, name="identity")
-        make_identity(nc, identity[:])
-        table = build_rotation_table(nc, keep)
+        table = build_rotation_table(nc, keep, reduced)
 
         x_codes = []
         x_planes = []
@@ -187,36 +220,38 @@ def tile_multiheadselfattention_pa_kernel(
             x_codes.append(codes)
             x_planes.append(plane)
 
-        pair_shape = [P, 2, TILE_HEADS, HALF, 2]
         for w, (words, scales, out) in enumerate(weights):
             out_rows = out.rearrange("b h (m j) d -> m (b h) (j d)", j=POS_TILES)
             for col_tile in range(COL_TILES):
-                words_tile = word_tiles[w * COL_TILES + col_tile]
-                columns = slice(col_tile * N_TILE, (col_tile + 1) * N_TILE)
                 rotated = results.tile([P, TILE_HEADS, POS_TILES, HEAD_DIM], F32, name="rotated")
-                terms = products.tile([P, POS_TILES] + pair_shape[1:], F32, name="terms")
+                terms = products.tile([P, POS_TILES, 2, TILE_HEADS, HALF, 2], F32, name="terms")
+                banks = []
                 for j in range(POS_TILES):
-                    sums = psum.tile([P, N_TILE], F32, name="sums", tag="bank")
-                    for g in range(PASSES):
-                        positions = slice(g * P, (g + 1) * P)
-                        nc.tensor.matmul_mx(
-                            out=sums[:],
-                            lhsT=x_codes[j][:, positions].bitcast(FP8X4),
-                            lhsT_scale=x_planes[j][:, positions],
-                            rhs=words_tile[:, g, :].bitcast(FP8X4),
-                            rhs_scale=plane_tiles[w][PLANE_ROWS * g : P, columns],
-                            start=(g == 0),
-                            stop=(g == PASSES - 1),
+                    bank = psum.tile([P, N_TILE], F32, name="bank", tag="bank")
+                    banks.append(bank)
+                for words_tile, offset, width in word_tiles[w * COL_TILES + col_tile]:
+                    columns = slice(col_tile * N_TILE + offset, col_tile * N_TILE + offset + width)
+                    piece_heads = slice(offset // HEAD_DIM, (offset + width) // HEAD_DIM)
+                    pair_shape = [P, 2, width // HEAD_DIM, HALF, 2]
+                    for j in range(POS_TILES):
+                        sums = banks[j][:, offset : offset + width]
+                        for g in range(PASSES):
+                            positions = slice(g * P, (g + 1) * P)
+                            nc.tensor.matmul_mx(
+                                out=sums,
+                                lhsT=x_codes[j][:, positions].bitcast(FP8X4),
+                                lhsT_scale=x_planes[j][:, positions],
+                                rhs=words_tile[:, g, :].bitcast(FP8X4),
+                                rhs_scale=plane_tiles[w][PLANE_ROWS * g : P, columns],
+                                start=(g == 0),
+                                stop=(g == PASSES - 1),
+                            )
+                        nc.vector.tensor_tensor(
+                            out=terms[:, j, :, piece_heads],
+                            in0=sums.rearrange("p (h i v) -> p v h i", i=HALF, v=2).unsqueeze(4).to_broadcast(pair_shape),
+                            in1=table[:, j].unsqueeze(2).to_broadcast(pair_shape),
+                            op=ALU.mult,
                         )
-                    nc.vector.tensor_tensor(
-                        out=terms[:, j],
-                        in0=sums[:]
-                        .rearrange("p (h i v) -> p v h i", h=TILE_HEADS, v=2)
-                        .unsqueeze(4)
-                        .to_broadcast(pair_shape),
-                        in1=table[:, j].unsqueeze(2).to_broadcast(pair_shape),
-                        op=ALU.mult,
-                    )
                 heads = slice(col_tile * TILE_HEADS, (col_tile + 1) * TILE_HEADS)
                 if w == len(weights) - 1 and col_tile == COL_TILES - 1:
                     for j in range(POS_TILES):

@@ -32,6 +32,7 @@ TILE_HEADS = N_TILE // HEAD_DIM
 COL_TILES = HEADS * HEAD_DIM // N_TILE
 PLANE_ROWS = 4
 QUADRANTS = 4
+FIRST_IDLE_MATMULS = 4
 
 TWO_PI = 2.0 * math.pi
 TWO_PI_HEAD = int(TWO_PI * 2.0**14) / 2.0**14
@@ -172,6 +173,14 @@ def tile_multiheadselfattention_pa_kernel(
         identity = keep.tile([P, P], F32, name="identity")
         make_identity(nc, identity[:])
 
+        idle_bank = psum.tile([P, P], F32, name="idle_bank", tag="bank")
+
+        def idle_matmul():
+            nc.tensor.matmul(out=idle_bank[:], lhsT=identity[:], rhs=identity[:], start=True, stop=True)
+
+        for count in range(FIRST_IDLE_MATMULS):
+            idle_matmul()
+
         plane_tiles = []
         for w in range(len(weights)):
             planes = keep.tile([P, HEADS * HEAD_DIM], U8, name="planes%d" % w, align_bytes=64)
@@ -210,6 +219,7 @@ def tile_multiheadselfattention_pa_kernel(
                             in_=pair_words[:, 2 * P * g + u : 2 * P * (g + 1) : 2],
                             identity=identity[:],
                         )
+                idle_matmul()
                 nc.scalar.copy(
                     out=grouped_words[:, first_pass : first_pass + 2, :, :],
                     in_=flipped[:].rearrange("p g u m -> p g m u"),

@@ -33,6 +33,7 @@ COL_TILES = HEADS * HEAD_DIM // N_TILE
 PLANE_ROWS = 4
 QUADRANTS = 4
 FIRST_IDLE_MATMULS = 4
+HALF_ADD_STEPS = 5
 
 TWO_PI = 2.0 * math.pi
 TWO_PI_HEAD = int(TWO_PI * 2.0**14) / 2.0**14
@@ -230,16 +231,29 @@ def tile_multiheadselfattention_pa_kernel(
             x_codes.append(codes)
             x_planes.append(plane)
 
+        def add_on_gpsimd(rotated, terms, tiles, heads):
+            nc.gpsimd.tensor_tensor(
+                out=rotated[:, heads, tiles, :].rearrange("p h j d -> p j h d"),
+                in0=terms[:, tiles, 0, heads].rearrange("p j h i e -> p j h (i e)"),
+                in1=terms[:, tiles, 1, heads].rearrange("p j h i e -> p j h (i e)"),
+                op=ALU.add,
+            )
+
+        all_tiles = slice(0, POS_TILES)
+        all_heads = slice(0, TILE_HEADS)
         for w, (words, scales, out) in enumerate(weights):
             out_rows = out.rearrange("b h (m j) d -> m (b h) (j d)", j=POS_TILES)
             for col_tile in range(COL_TILES):
+                step = w * COL_TILES + col_tile
+                last_step = step == len(weights) * COL_TILES - 1
                 rotated = results.tile([P, TILE_HEADS, POS_TILES, HEAD_DIM], F32, name="rotated")
                 terms = products.tile([P, POS_TILES, 2, TILE_HEADS, HALF, 2], F32, name="terms")
                 banks = []
                 for j in range(POS_TILES):
                     bank = psum.tile([P, N_TILE], F32, name="bank", tag="bank")
                     banks.append(bank)
-                for words_tile, offset, width in word_tiles[w * COL_TILES + col_tile]:
+                pieces = word_tiles[step]
+                for words_tile, offset, width in pieces:
                     columns = slice(col_tile * N_TILE + offset, col_tile * N_TILE + offset + width)
                     piece_heads = slice(offset // HEAD_DIM, (offset + width) // HEAD_DIM)
                     pair_shape = [P, 2, width // HEAD_DIM, HALF, 2]
@@ -262,8 +276,12 @@ def tile_multiheadselfattention_pa_kernel(
                             in1=table[:, j].unsqueeze(2).to_broadcast(pair_shape),
                             op=ALU.mult,
                         )
+                        if len(pieces) == 1 and step < HALF_ADD_STEPS and j % 2 == 1:
+                            add_on_gpsimd(rotated, terms, slice(j - 1, j + 1), all_heads)
+                    if len(pieces) > 1:
+                        add_on_gpsimd(rotated, terms, all_tiles, piece_heads)
                 heads = slice(col_tile * TILE_HEADS, (col_tile + 1) * TILE_HEADS)
-                if w == len(weights) - 1 and col_tile == COL_TILES - 1:
+                if last_step:
                     for j in range(POS_TILES):
                         nc.vector.tensor_tensor(
                             out=rotated[:, :, j, :],
@@ -275,10 +293,6 @@ def tile_multiheadselfattention_pa_kernel(
                             out=out_rows[:, heads, j * HEAD_DIM : (j + 1) * HEAD_DIM], in_=rotated[:, :, j, :]
                         )
                 else:
-                    nc.gpsimd.tensor_tensor(
-                        out=rotated[:].rearrange("p h j d -> p j h d"),
-                        in0=terms[:, :, 0].rearrange("p j h i e -> p j h (i e)"),
-                        in1=terms[:, :, 1].rearrange("p j h i e -> p j h (i e)"),
-                        op=ALU.add,
-                    )
+                    if step >= HALF_ADD_STEPS:
+                        add_on_gpsimd(rotated, terms, all_tiles, all_heads)
                     nc.scalar.dma_start(out=out_rows[:, heads, :], in_=rotated[:].rearrange("m h j d -> m h (j d)"))

@@ -234,8 +234,8 @@ def tile_multiheadselfattention_pa_kernel(
         def add_on_gpsimd(rotated, terms, tiles, heads):
             nc.gpsimd.tensor_tensor(
                 out=rotated[:, heads, tiles, :].rearrange("p h j d -> p j h d"),
-                in0=terms[:, tiles, 0, heads].rearrange("p j h i e -> p j h (i e)"),
-                in1=terms[:, tiles, 1, heads].rearrange("p j h i e -> p j h (i e)"),
+                in0=terms[:, tiles, 0].rearrange("p j h i e -> p j h (i e)"),
+                in1=terms[:, tiles, 1].rearrange("p j h i e -> p j h (i e)"),
                 op=ALU.add,
             )
 
@@ -247,7 +247,6 @@ def tile_multiheadselfattention_pa_kernel(
                 step = w * COL_TILES + col_tile
                 last_step = step == len(weights) * COL_TILES - 1
                 rotated = results.tile([P, TILE_HEADS, POS_TILES, HEAD_DIM], F32, name="rotated")
-                terms = products.tile([P, POS_TILES, 2, TILE_HEADS, HALF, 2], F32, name="terms")
                 banks = []
                 for j in range(POS_TILES):
                     bank = psum.tile([P, N_TILE], F32, name="bank", tag="bank")
@@ -257,6 +256,7 @@ def tile_multiheadselfattention_pa_kernel(
                     columns = slice(col_tile * N_TILE + offset, col_tile * N_TILE + offset + width)
                     piece_heads = slice(offset // HEAD_DIM, (offset + width) // HEAD_DIM)
                     pair_shape = [P, 2, width // HEAD_DIM, HALF, 2]
+                    terms = products.tile([P, POS_TILES, 2, width // HEAD_DIM, HALF, 2], F32, name="terms")
                     for j in range(POS_TILES):
                         sums = banks[j][:, offset : offset + width]
                         for g in range(PASSES):
@@ -271,7 +271,7 @@ def tile_multiheadselfattention_pa_kernel(
                                 stop=(g == PASSES - 1),
                             )
                         nc.vector.tensor_tensor(
-                            out=terms[:, j, :, piece_heads],
+                            out=terms[:, j],
                             in0=sums.rearrange("p (h i v) -> p v h i", i=HALF, v=2).unsqueeze(4).to_broadcast(pair_shape),
                             in1=table[:, j].unsqueeze(2).to_broadcast(pair_shape),
                             op=ALU.mult,

@@ -33,7 +33,7 @@ COL_TILES = HEADS * HEAD_DIM // N_TILE
 PLANE_ROWS = 4
 QUADRANTS = 4
 FIRST_IDLE_MATMULS = 4
-HALF_ADD_STEPS = 5
+GPSIMD_LAST_TILES = 2
 
 TWO_PI = 2.0 * math.pi
 TWO_PI_HEAD = int(TWO_PI * 2.0**14) / 2.0**14
@@ -276,23 +276,26 @@ def tile_multiheadselfattention_pa_kernel(
                             in1=table[:, j].unsqueeze(2).to_broadcast(pair_shape),
                             op=ALU.mult,
                         )
-                        if len(pieces) == 1 and step < HALF_ADD_STEPS and j % 2 == 1:
+                        if len(pieces) == 1 and j % 2 == 1 and (not last_step or j < GPSIMD_LAST_TILES):
                             add_on_gpsimd(rotated, terms, slice(j - 1, j + 1), all_heads)
                     if len(pieces) > 1:
                         add_on_gpsimd(rotated, terms, all_tiles, piece_heads)
                 heads = slice(col_tile * TILE_HEADS, (col_tile + 1) * TILE_HEADS)
                 if last_step:
-                    for j in range(POS_TILES):
+                    nc.scalar.dma_start(
+                        out=out_rows[:, heads, 0 : GPSIMD_LAST_TILES * HEAD_DIM],
+                        in_=rotated[:, :, 0:GPSIMD_LAST_TILES, :].rearrange("m h j d -> m h (j d)"),
+                    )
+                    rotated_last = results.tile([P, TILE_HEADS, POS_TILES, HEAD_DIM], F32, name="rotated")
+                    for j in range(GPSIMD_LAST_TILES, POS_TILES):
                         nc.vector.tensor_tensor(
-                            out=rotated[:, :, j, :],
+                            out=rotated_last[:, :, j, :],
                             in0=terms[:, j, 0].rearrange("p h i e -> p h (i e)"),
                             in1=terms[:, j, 1].rearrange("p h i e -> p h (i e)"),
                             op=ALU.add,
                         )
                         nc.sync.dma_start(
-                            out=out_rows[:, heads, j * HEAD_DIM : (j + 1) * HEAD_DIM], in_=rotated[:, :, j, :]
+                            out=out_rows[:, heads, j * HEAD_DIM : (j + 1) * HEAD_DIM], in_=rotated_last[:, :, j, :]
                         )
                 else:
-                    if step >= HALF_ADD_STEPS:
-                        add_on_gpsimd(rotated, terms, all_tiles, all_heads)
                     nc.scalar.dma_start(out=out_rows[:, heads, :], in_=rotated[:].rearrange("m h j d -> m h (j d)"))

@@ -32,7 +32,7 @@ TILE_HEADS = N_TILE // HEAD_DIM
 COL_TILES = HEADS * HEAD_DIM // N_TILE
 PLANE_ROWS = 4
 QUADRANTS = 4
-FIRST_IDLE_MATMULS = 4
+FIRST_IDLE_MATMULS = 3
 GPSIMD_LAST_TILES = 2
 
 TWO_PI = 2.0 * math.pi
@@ -101,13 +101,17 @@ def build_reduced_angles(nc, pool):
     return reduced
 
 
-def build_rotation_table(nc, pool, reduced):
+def take_sines(nc, pool, reduced):
     shape = [P, POS_TILES, HALF]
     sin_half = pool.tile(shape, F32, name="sin_half")
     sin_quarter = pool.tile(shape, F32, name="sin_quarter")
     nc.scalar.activation(out=sin_quarter[:], in_=reduced[:], func=ACT.Sin, scale=0.25)
     nc.scalar.activation(out=sin_half[:], in_=reduced[:], func=ACT.Sin, scale=0.5)
+    return sin_half, sin_quarter
 
+
+def build_rotation_table(nc, pool, sin_half, sin_quarter):
+    shape = [P, POS_TILES, HALF]
     cos_half_less_1 = pool.tile(shape, F32, name="cos_half_less_1")
     half_sin = pool.tile(shape, F32, name="half_sin")
     cos_less_1 = pool.tile(shape, F32, name="cos_less_1")
@@ -128,12 +132,12 @@ def build_rotation_table(nc, pool, reduced):
     return table
 
 
-def load_scale_planes(nc, planes, scales):
+def load_scale_planes(nc, planes, scales, first, width):
     for quadrant in range(QUADRANTS):
-        first = 32 * quadrant
+        row = 32 * quadrant
         nc.sync.dma_start(
-            out=planes[first : first + PASSES * PLANE_ROWS, :].bitcast(I32),
-            in_=scales[:, PLANE_ROWS * quadrant : PLANE_ROWS * (quadrant + 1), :].bitcast(I32),
+            out=planes[row : row + PASSES * PLANE_ROWS, first : first + width].bitcast(I32),
+            in_=scales[:, PLANE_ROWS * quadrant : PLANE_ROWS * (quadrant + 1), first : first + width].bitcast(I32),
         )
 
 
@@ -144,8 +148,8 @@ def load_weight_columns(nc, words_tile, words, first, width):
     )
 
 
-def column_pieces(w, col_tile):
-    if w == 0 and col_tile == 0:
+def column_pieces(step):
+    if step == 0:
         return [N_TILE // 2, N_TILE // 2]
     return [N_TILE]
 
@@ -155,6 +159,8 @@ def tile_multiheadselfattention_pa_kernel(
 ):
     nc = tc.nc
     weights = [(Wq_words, Wq_scales, out_0), (Wk_words, Wk_scales, out_1)]
+    steps = len(weights) * COL_TILES
+    columns_of_a_weight = HEADS * HEAD_DIM
 
     with tc.manual_schedule(), tc.tile_pool(name="keep", bufs=1) as keep, tc.tile_pool(
         name="products", bufs=3
@@ -163,13 +169,42 @@ def tile_multiheadselfattention_pa_kernel(
         x_tiles = []
         for j in range(POS_TILES):
             x_tile = keep.tile([P, EMB], BF16, name="x%d" % j)
-            nc.sync.dma_start(out=x_tile[:], in_=x_rows[:, j, :])
             x_tiles.append(x_tile)
+        plane_tiles = []
+        for w in range(len(weights)):
+            planes = keep.tile([P, columns_of_a_weight], U8, name="planes%d" % w, align_bytes=64)
+            plane_tiles.append(planes)
+        word_tiles = []
+        for step in range(steps):
+            piece_tiles = []
+            offset = 0
+            for width in column_pieces(step):
+                words_tile = keep.tile([P, PASSES, width], U32, name="w%d_%d" % (step, offset), align_bytes=64)
+                piece_tiles.append((words_tile, offset, width))
+                offset += width
+            word_tiles.append(piece_tiles)
 
+        def load_x(j):
+            nc.sync.dma_start(out=x_tiles[j][:], in_=x_rows[:, j, :])
+
+        def load_words(step):
+            for words_tile, offset, width in word_tiles[step]:
+                load_weight_columns(
+                    nc, words_tile, weights[step // COL_TILES][0], (step % COL_TILES) * N_TILE + offset, width
+                )
+
+        load_x(0)
+        load_x(1)
         zero = keep.tile([P, 1], F32, name="zero")
         warm = keep.tile([P, 1], F32, name="warm")
         nc.vector.memset(zero[:], 0.0)
         nc.scalar.activation(out=warm[:], in_=zero[:], func=ACT.Sin)
+        nc.vector.memset(plane_tiles[0][:, 0:N_TILE].bitcast(I32), 0)
+        load_scale_planes(nc, plane_tiles[0], Wq_scales, 0, N_TILE)
+        load_words(0)
+        load_x(2)
+        load_x(3)
+
         reduced = build_reduced_angles(nc, keep)
         identity = keep.tile([P, P], F32, name="identity")
         make_identity(nc, identity[:])
@@ -182,32 +217,20 @@ def tile_multiheadselfattention_pa_kernel(
         for count in range(FIRST_IDLE_MATMULS):
             idle_matmul()
 
-        plane_tiles = []
-        for w in range(len(weights)):
-            planes = keep.tile([P, HEADS * HEAD_DIM], U8, name="planes%d" % w, align_bytes=64)
-            nc.vector.memset(planes[:].bitcast(I32), 0)
-            plane_tiles.append(planes)
+        nc.vector.memset(plane_tiles[0][:, N_TILE:columns_of_a_weight].bitcast(I32), 0)
+        nc.vector.memset(plane_tiles[1][:].bitcast(I32), 0)
+        load_scale_planes(nc, plane_tiles[0], Wq_scales, N_TILE, columns_of_a_weight - N_TILE)
+        for step in range(1, COL_TILES):
+            load_words(step)
+        load_scale_planes(nc, plane_tiles[1], Wk_scales, 0, columns_of_a_weight)
+        for step in range(COL_TILES, steps):
+            load_words(step)
 
-        word_tiles = []
-        for w, (words, scales, out) in enumerate(weights):
-            load_scale_planes(nc, plane_tiles[w], scales)
-            for col_tile in range(COL_TILES):
-                piece_tiles = []
-                offset = 0
-                for width in column_pieces(w, col_tile):
-                    words_tile = keep.tile(
-                        [P, PASSES, width], U32, name="w%d_%d_%d" % (w, col_tile, offset), align_bytes=64
-                    )
-                    load_weight_columns(nc, words_tile, words, col_tile * N_TILE + offset, width)
-                    piece_tiles.append((words_tile, offset, width))
-                    offset += width
-                word_tiles.append(piece_tiles)
+        grouped_tiles = {}
+        x_codes = {}
+        x_planes = {}
 
-        table = build_rotation_table(nc, keep, reduced)
-
-        x_codes = []
-        x_planes = []
-        for j in range(POS_TILES):
+        def transpose_x(j, idle_matmuls):
             pair_words = x_tiles[j][:].bitcast(F32)
             grouped = keep.tile([P, PASSES * P * PACK], BF16, name="grouped%d" % j, align_bytes=64)
             grouped_words = grouped[:].bitcast(F32).rearrange("p (g m u) -> p g m u", g=PASSES, u=2)
@@ -220,82 +243,107 @@ def tile_multiheadselfattention_pa_kernel(
                             in_=pair_words[:, 2 * P * g + u : 2 * P * (g + 1) : 2],
                             identity=identity[:],
                         )
-                idle_matmul()
+                if idle_matmuls:
+                    idle_matmul()
                 nc.scalar.copy(
                     out=grouped_words[:, first_pass : first_pass + 2, :, :],
                     in_=flipped[:].rearrange("p g u m -> p g m u"),
                 )
+            grouped_tiles[j] = grouped
+
+        def quantize_x(j):
             codes = keep.tile([P, PASSES * P], U32, name="x_codes%d" % j, align_bytes=64)
             plane = keep.tile([P, PASSES * P], U8, name="x_plane%d" % j, align_bytes=64)
-            nc.vector.quantize_mx(out=codes[:].bitcast(FP8X4), scales=plane[:], in_=grouped[:])
-            x_codes.append(codes)
-            x_planes.append(plane)
+            nc.vector.quantize_mx(out=codes[:].bitcast(FP8X4), scales=plane[:], in_=grouped_tiles[j][:])
+            x_codes[j] = codes
+            x_planes[j] = plane
 
-        def add_on_gpsimd(rotated, terms, tiles, heads):
-            nc.gpsimd.tensor_tensor(
-                out=rotated[:, heads, tiles, :].rearrange("p h j d -> p j h d"),
-                in0=terms[:, tiles, 0].rearrange("p j h i e -> p j h (i e)"),
-                in1=terms[:, tiles, 1].rearrange("p j h i e -> p j h (i e)"),
-                op=ALU.add,
-            )
+        pair_shape = [P, 2, TILE_HEADS, HALF, 2]
+        step_tiles = {}
 
-        all_tiles = slice(0, POS_TILES)
-        all_heads = slice(0, TILE_HEADS)
-        for w, (words, scales, out) in enumerate(weights):
+        def open_step(step):
+            rotated = results.tile([P, TILE_HEADS, POS_TILES, HEAD_DIM], F32, name="rotated")
+            terms = products.tile([P, POS_TILES, 2, TILE_HEADS, HALF, 2], F32, name="terms")
+            step_tiles[step] = (rotated, terms)
+
+        def project(step, j):
+            w = step // COL_TILES
+            first = (step % COL_TILES) * N_TILE
+            bank = psum.tile([P, N_TILE], F32, name="bank", tag="bank")
+            for words_tile, offset, width in word_tiles[step]:
+                for g in range(PASSES):
+                    positions = slice(g * P, (g + 1) * P)
+                    nc.tensor.matmul_mx(
+                        out=bank[:, offset : offset + width],
+                        lhsT=x_codes[j][:, positions].bitcast(FP8X4),
+                        lhsT_scale=x_planes[j][:, positions],
+                        rhs=words_tile[:, g, :].bitcast(FP8X4),
+                        rhs_scale=plane_tiles[w][PLANE_ROWS * g : P, first + offset : first + offset + width],
+                        start=(g == 0),
+                        stop=(g == PASSES - 1),
+                    )
+            return bank
+
+        def rotate(step, j, bank):
+            rotated, terms = step_tiles[step]
+            out = weights[step // COL_TILES][2]
             out_rows = out.rearrange("b h (m j) d -> m (b h) (j d)", j=POS_TILES)
-            for col_tile in range(COL_TILES):
-                step = w * COL_TILES + col_tile
-                last_step = step == len(weights) * COL_TILES - 1
-                rotated = results.tile([P, TILE_HEADS, POS_TILES, HEAD_DIM], F32, name="rotated")
-                banks = []
-                for j in range(POS_TILES):
-                    bank = psum.tile([P, N_TILE], F32, name="bank", tag="bank")
-                    banks.append(bank)
-                pieces = word_tiles[step]
-                for words_tile, offset, width in pieces:
-                    columns = slice(col_tile * N_TILE + offset, col_tile * N_TILE + offset + width)
-                    piece_heads = slice(offset // HEAD_DIM, (offset + width) // HEAD_DIM)
-                    pair_shape = [P, 2, width // HEAD_DIM, HALF, 2]
-                    terms = products.tile([P, POS_TILES, 2, width // HEAD_DIM, HALF, 2], F32, name="terms")
-                    for j in range(POS_TILES):
-                        sums = banks[j][:, offset : offset + width]
-                        for g in range(PASSES):
-                            positions = slice(g * P, (g + 1) * P)
-                            nc.tensor.matmul_mx(
-                                out=sums,
-                                lhsT=x_codes[j][:, positions].bitcast(FP8X4),
-                                lhsT_scale=x_planes[j][:, positions],
-                                rhs=words_tile[:, g, :].bitcast(FP8X4),
-                                rhs_scale=plane_tiles[w][PLANE_ROWS * g : P, columns],
-                                start=(g == 0),
-                                stop=(g == PASSES - 1),
-                            )
-                        nc.vector.tensor_tensor(
-                            out=terms[:, j],
-                            in0=sums.rearrange("p (h i v) -> p v h i", i=HALF, v=2).unsqueeze(4).to_broadcast(pair_shape),
-                            in1=table[:, j].unsqueeze(2).to_broadcast(pair_shape),
-                            op=ALU.mult,
-                        )
-                        if len(pieces) == 1 and j % 2 == 1 and (not last_step or j < GPSIMD_LAST_TILES):
-                            add_on_gpsimd(rotated, terms, slice(j - 1, j + 1), all_heads)
-                    if len(pieces) > 1:
-                        add_on_gpsimd(rotated, terms, all_tiles, piece_heads)
-                heads = slice(col_tile * TILE_HEADS, (col_tile + 1) * TILE_HEADS)
-                if last_step:
+            first_head = (step % COL_TILES) * TILE_HEADS
+            heads = slice(first_head, first_head + TILE_HEADS)
+            nc.vector.tensor_tensor(
+                out=terms[:, j],
+                in0=bank[:].rearrange("p (h i v) -> p v h i", i=HALF, v=2).unsqueeze(4).to_broadcast(pair_shape),
+                in1=table[:, j].unsqueeze(2).to_broadcast(pair_shape),
+                op=ALU.mult,
+            )
+            if j % 2 == 0:
+                return
+            if step < steps - 1 or j < GPSIMD_LAST_TILES:
+                both = slice(j - 1, j + 1)
+                nc.gpsimd.tensor_tensor(
+                    out=rotated[:, :, both, :].rearrange("p h j d -> p j h d"),
+                    in0=terms[:, both, 0].rearrange("p j h i e -> p j h (i e)"),
+                    in1=terms[:, both, 1].rearrange("p j h i e -> p j h (i e)"),
+                    op=ALU.add,
+                )
+                if step == steps - 1:
                     nc.scalar.dma_start(
                         out=out_rows[:, heads, 0 : GPSIMD_LAST_TILES * HEAD_DIM],
                         in_=rotated[:, :, 0:GPSIMD_LAST_TILES, :].rearrange("m h j d -> m h (j d)"),
                     )
-                    rotated_last = results.tile([P, TILE_HEADS, POS_TILES, HEAD_DIM], F32, name="rotated")
-                    for j in range(GPSIMD_LAST_TILES, POS_TILES):
-                        nc.vector.tensor_tensor(
-                            out=rotated_last[:, :, j, :],
-                            in0=terms[:, j, 0].rearrange("p h i e -> p h (i e)"),
-                            in1=terms[:, j, 1].rearrange("p h i e -> p h (i e)"),
-                            op=ALU.add,
-                        )
-                        nc.sync.dma_start(
-                            out=out_rows[:, heads, j * HEAD_DIM : (j + 1) * HEAD_DIM], in_=rotated_last[:, :, j, :]
-                        )
-                else:
+                elif j == POS_TILES - 1:
                     nc.scalar.dma_start(out=out_rows[:, heads, :], in_=rotated[:].rearrange("m h j d -> m h (j d)"))
+                return
+            rotated_last = results.tile([P, TILE_HEADS, POS_TILES, HEAD_DIM], F32, name="rotated")
+            for late in range(j - 1, j + 1):
+                nc.vector.tensor_tensor(
+                    out=rotated_last[:, :, late, :],
+                    in0=terms[:, late, 0].rearrange("p h i e -> p h (i e)"),
+                    in1=terms[:, late, 1].rearrange("p h i e -> p h (i e)"),
+                    op=ALU.add,
+                )
+                nc.sync.dma_start(
+                    out=out_rows[:, heads, late * HEAD_DIM : (late + 1) * HEAD_DIM], in_=rotated_last[:, :, late, :]
+                )
+
+        transpose_x(0, True)
+        transpose_x(1, True)
+        quantize_x(0)
+        quantize_x(1)
+        sin_half, sin_quarter = take_sines(nc, keep, reduced)
+        table = build_rotation_table(nc, keep, sin_half, sin_quarter)
+        open_step(0)
+        bank_0 = project(0, 0)
+        transpose_x(2, False)
+        bank_1 = project(0, 1)
+        transpose_x(3, False)
+        quantize_x(2)
+        rotate(0, 0, bank_0)
+        quantize_x(3)
+        rotate(0, 1, bank_1)
+        for j in range(2, POS_TILES):
+            rotate(0, j, project(0, j))
+        for step in range(1, steps):
+            open_step(step)
+            for j in range(POS_TILES):
+                rotate(step, j, project(step, j))

@@ -184,28 +184,30 @@ def tile_multiheadselfattention_pa_kernel(
                 offset += width
             word_tiles.append(piece_tiles)
 
-        def load_x(j):
-            nc.sync.dma_start(out=x_tiles[j][:], in_=x_rows[:, j, :])
+        def load_x(j, pieces):
+            width = EMB // pieces
+            for first in range(0, EMB, width):
+                nc.sync.dma_start(out=x_tiles[j][:, first : first + width], in_=x_rows[:, j, first : first + width])
 
-        def load_words(step):
-            for words_tile, offset, width in word_tiles[step]:
-                load_weight_columns(
-                    nc, words_tile, weights[step // COL_TILES][0], (step % COL_TILES) * N_TILE + offset, width
-                )
+        def load_words(step, piece):
+            words_tile, offset, width = word_tiles[step][piece]
+            load_weight_columns(
+                nc, words_tile, weights[step // COL_TILES][0], (step % COL_TILES) * N_TILE + offset, width
+            )
 
-        load_x(0)
-        load_x(1)
+        load_x(0, 2)
+        load_x(1, 1)
         zero = keep.tile([P, 1], F32, name="zero")
         warm = keep.tile([P, 1], F32, name="warm")
         nc.vector.memset(zero[:], 0.0)
         nc.scalar.activation(out=warm[:], in_=zero[:], func=ACT.Sin)
         nc.vector.memset(plane_tiles[0][:, 0:N_TILE].bitcast(I32), 0)
         load_scale_planes(nc, plane_tiles[0], Wq_scales, 0, N_TILE)
-        load_words(0)
-        load_x(2)
-        load_x(3)
+        load_words(0, 0)
+        load_x(2, 1)
+        load_x(3, 1)
+        load_words(0, 1)
 
-        reduced = build_reduced_angles(nc, keep)
         identity = keep.tile([P, P], F32, name="identity")
         make_identity(nc, identity[:])
 
@@ -217,14 +219,16 @@ def tile_multiheadselfattention_pa_kernel(
         for count in range(FIRST_IDLE_MATMULS):
             idle_matmul()
 
+        reduced = build_reduced_angles(nc, keep)
+
         nc.vector.memset(plane_tiles[0][:, N_TILE:columns_of_a_weight].bitcast(I32), 0)
         nc.vector.memset(plane_tiles[1][:].bitcast(I32), 0)
         load_scale_planes(nc, plane_tiles[0], Wq_scales, N_TILE, columns_of_a_weight - N_TILE)
         for step in range(1, COL_TILES):
-            load_words(step)
+            load_words(step, 0)
         load_scale_planes(nc, plane_tiles[1], Wk_scales, 0, columns_of_a_weight)
         for step in range(COL_TILES, steps):
-            load_words(step)
+            load_words(step, 0)
 
         grouped_tiles = {}
         x_codes = {}
@@ -266,22 +270,26 @@ def tile_multiheadselfattention_pa_kernel(
             terms = products.tile([P, POS_TILES, 2, TILE_HEADS, HALF, 2], F32, name="terms")
             step_tiles[step] = (rotated, terms)
 
-        def project(step, j):
+        def project_piece(step, j, bank, piece):
             w = step // COL_TILES
             first = (step % COL_TILES) * N_TILE
+            words_tile, offset, width = word_tiles[step][piece]
+            for g in range(PASSES):
+                positions = slice(g * P, (g + 1) * P)
+                nc.tensor.matmul_mx(
+                    out=bank[:, offset : offset + width],
+                    lhsT=x_codes[j][:, positions].bitcast(FP8X4),
+                    lhsT_scale=x_planes[j][:, positions],
+                    rhs=words_tile[:, g, :].bitcast(FP8X4),
+                    rhs_scale=plane_tiles[w][PLANE_ROWS * g : P, first + offset : first + offset + width],
+                    start=(g == 0),
+                    stop=(g == PASSES - 1),
+                )
+
+        def project(step, j):
             bank = psum.tile([P, N_TILE], F32, name="bank", tag="bank")
-            for words_tile, offset, width in word_tiles[step]:
-                for g in range(PASSES):
-                    positions = slice(g * P, (g + 1) * P)
-                    nc.tensor.matmul_mx(
-                        out=bank[:, offset : offset + width],
-                        lhsT=x_codes[j][:, positions].bitcast(FP8X4),
-                        lhsT_scale=x_planes[j][:, positions],
-                        rhs=words_tile[:, g, :].bitcast(FP8X4),
-                        rhs_scale=plane_tiles[w][PLANE_ROWS * g : P, first + offset : first + offset + width],
-                        start=(g == 0),
-                        stop=(g == PASSES - 1),
-                    )
+            for piece in range(len(word_tiles[step])):
+                project_piece(step, j, bank, piece)
             return bank
 
         def rotate(step, j, bank):
@@ -333,13 +341,17 @@ def tile_multiheadselfattention_pa_kernel(
         sin_half, sin_quarter = take_sines(nc, keep, reduced)
         table = build_rotation_table(nc, keep, sin_half, sin_quarter)
         open_step(0)
-        bank_0 = project(0, 0)
+        bank_0 = psum.tile([P, N_TILE], F32, name="bank", tag="bank")
+        project_piece(0, 0, bank_0, 0)
         transpose_x(2, False)
-        bank_1 = project(0, 1)
+        bank_1 = psum.tile([P, N_TILE], F32, name="bank", tag="bank")
+        project_piece(0, 1, bank_1, 0)
         transpose_x(3, False)
         quantize_x(2)
-        rotate(0, 0, bank_0)
         quantize_x(3)
+        project_piece(0, 0, bank_0, 1)
+        rotate(0, 0, bank_0)
+        project_piece(0, 1, bank_1, 1)
         rotate(0, 1, bank_1)
         for j in range(2, POS_TILES):
             rotate(0, j, project(0, j))

@@ -172,14 +172,14 @@ def tile_multiheadselfattention_pa_kernel(
             x_tiles.append(x_tile)
         plane_tiles = []
         for w in range(len(weights)):
-            planes = keep.tile([P, columns_of_a_weight], U8, name="planes%d" % w, align_bytes=64)
+            planes = keep.tile([P, columns_of_a_weight], U8, name="planes%d" % w, align_bytes=256)
             plane_tiles.append(planes)
         word_tiles = []
         for step in range(steps):
             piece_tiles = []
             offset = 0
             for width in column_pieces(step):
-                words_tile = keep.tile([P, PASSES, width], U32, name="w%d_%d" % (step, offset), align_bytes=64)
+                words_tile = keep.tile([P, PASSES, width], U32, name="w%d_%d" % (step, offset), align_bytes=256)
                 piece_tiles.append((words_tile, offset, width))
                 offset += width
             word_tiles.append(piece_tiles)
@@ -256,8 +256,8 @@ def tile_multiheadselfattention_pa_kernel(
             grouped_tiles[j] = grouped
 
         def quantize_x(j):
-            codes = keep.tile([P, PASSES * P], U32, name="x_codes%d" % j, align_bytes=64)
-            plane = keep.tile([P, PASSES * P], U8, name="x_plane%d" % j, align_bytes=64)
+            codes = keep.tile([P, PASSES * P], U32, name="x_codes%d" % j, align_bytes=256)
+            plane = keep.tile([P, PASSES * P], U8, name="x_plane%d" % j, align_bytes=256)
             nc.vector.quantize_mx(out=codes[:].bitcast(FP8X4), scales=plane[:], in_=grouped_tiles[j][:])
             x_codes[j] = codes
             x_planes[j] = plane

@@ -223,8 +223,10 @@ def tile_multiheadselfattention_pa_kernel(
 
         nc.vector.memset(plane_tiles[0][:, N_TILE:columns_of_a_weight].bitcast(I32), 0)
         nc.vector.memset(plane_tiles[1][:].bitcast(I32), 0)
-        load_scale_planes(nc, plane_tiles[0], Wq_scales, N_TILE, columns_of_a_weight - N_TILE)
-        for step in range(1, COL_TILES):
+        load_scale_planes(nc, plane_tiles[0], Wq_scales, N_TILE, N_TILE)
+        load_words(1, 0)
+        load_scale_planes(nc, plane_tiles[0], Wq_scales, 2 * N_TILE, columns_of_a_weight - 2 * N_TILE)
+        for step in range(2, COL_TILES):
             load_words(step, 0)
         load_scale_planes(nc, plane_tiles[1], Wk_scales, 0, columns_of_a_weight)
         for step in range(COL_TILES, steps):

@@ -36,17 +36,12 @@ FIRST_IDLE_MATMULS = 3
 GPSIMD_LAST_TILES = 2
 
 TWO_PI = 2.0 * math.pi
-TWO_PI_HEAD = int(TWO_PI * 2.0**14) / 2.0**14
-TWO_PI_TAIL = TWO_PI - TWO_PI_HEAD
 ROUND_MAGIC = 1.5 * 2.0**23
 
 FLOPS = 2 * SEQ * EMB * 2 * HEADS * HEAD_DIM
 
 
-def build_reduced_angles(nc, pool):
-    position_int = pool.tile([P, POS_TILES], I32, name="position_int")
-    nc.gpsimd.iota(position_int[:], pattern=[[1, POS_TILES]], base=0, channel_multiplier=POS_TILES)
-
+def build_turn_fractions(nc, pool, position):
     powers = pool.tile([P, DIGITS, RADIX], F32, name="powers")
     nc.vector.memset(powers[:], 1.0)
     for digit in range(DIGITS):
@@ -56,8 +51,6 @@ def build_reduced_angles(nc, pool):
                 in0=powers[:, digit, 0:1],
                 scalar1=ROPE_BASE ** (-2.0 * c * RADIX**digit / HEAD_DIM),
             )
-    position = pool.tile([P, POS_TILES], F32, name="position")
-    nc.vector.tensor_copy(out=position[:], in_=position_int[:])
 
     square = [P, RADIX, RADIX]
     low = pool.tile(square, F32, name="low")
@@ -68,11 +61,13 @@ def build_reduced_angles(nc, pool):
         op=ALU.mult,
     )
     high = pool.tile([P, POS_TILES, RADIX], F32, name="high")
-    nc.vector.tensor_tensor(
+    nc.vector.scalar_tensor_tensor(
         out=high[:],
         in0=position[:].unsqueeze(2).to_broadcast([P, POS_TILES, RADIX]),
+        scalar=1.0 / TWO_PI,
         in1=powers[:, 2, :].unsqueeze(1).to_broadcast([P, POS_TILES, RADIX]),
-        op=ALU.mult,
+        op0=ALU.mult,
+        op1=ALU.mult,
     )
     shape = [P, POS_TILES, HALF]
     outer = [P, POS_TILES * RADIX, RADIX * RADIX]
@@ -85,51 +80,51 @@ def build_reduced_angles(nc, pool):
     )
 
     shifted = pool.tile(shape, F32, name="shifted")
-    turns = pool.tile(shape, F32, name="turns")
-    coarse = pool.tile(shape, F32, name="coarse")
-    reduced = pool.tile(shape, F32, name="reduced")
-    nc.vector.tensor_scalar(
-        out=shifted[:], in0=angle[:], scalar1=1.0 / TWO_PI, scalar2=ROUND_MAGIC, op0=ALU.mult, op1=ALU.add
-    )
-    nc.vector.tensor_scalar_sub(out=turns[:], in0=shifted[:], scalar1=ROUND_MAGIC)
+    minus_fraction = pool.tile(shape, F32, name="minus_fraction")
+    nc.vector.tensor_scalar_add(out=shifted[:], in0=angle[:], scalar1=ROUND_MAGIC)
     nc.vector.scalar_tensor_tensor(
-        out=coarse[:], in0=turns[:], scalar=-TWO_PI_HEAD, in1=angle[:], op0=ALU.mult, op1=ALU.add
+        out=minus_fraction[:], in0=shifted[:], scalar=ROUND_MAGIC, in1=angle[:], op0=ALU.subtract, op1=ALU.subtract
     )
-    nc.vector.scalar_tensor_tensor(
-        out=reduced[:], in0=turns[:], scalar=-TWO_PI_TAIL, in1=coarse[:], op0=ALU.mult, op1=ALU.add
-    )
-    return reduced
+    return minus_fraction
 
 
-def take_sines(nc, pool, reduced):
-    shape = [P, POS_TILES, HALF]
-    sin_half = pool.tile(shape, F32, name="sin_half")
-    sin_quarter = pool.tile(shape, F32, name="sin_quarter")
-    nc.scalar.activation(out=sin_quarter[:], in_=reduced[:], func=ACT.Sin, scale=0.25)
-    nc.scalar.activation(out=sin_half[:], in_=reduced[:], func=ACT.Sin, scale=0.5)
-    return sin_half, sin_quarter
+def take_sine(nc, pool, minus_fraction, part, name):
+    sine = pool.tile([P, POS_TILES, HALF], F32, name=name)
+    nc.scalar.activation(out=sine[:], in_=minus_fraction[:], func=ACT.Sin, scale=-TWO_PI / part)
+    return sine
 
 
-def build_rotation_table(nc, pool, sin_half, sin_quarter):
+def rotation_table(nc, pool):
     shape = [P, POS_TILES, HALF]
     cos_half_less_1 = pool.tile(shape, F32, name="cos_half_less_1")
     half_sin = pool.tile(shape, F32, name="half_sin")
     cos_less_1 = pool.tile(shape, F32, name="cos_less_1")
     table = pool.tile([P, POS_TILES, 2, HALF, 2], F32, name="table")
-    nc.vector.scalar_tensor_tensor(
-        out=cos_half_less_1[:], in0=sin_quarter[:], scalar=-2.0, in1=sin_quarter[:], op0=ALU.mult, op1=ALU.mult
-    )
-    nc.vector.scalar_tensor_tensor(
-        out=cos_less_1[:], in0=sin_half[:], scalar=-2.0, in1=sin_half[:], op0=ALU.mult, op1=ALU.mult
-    )
-    nc.vector.scalar_tensor_tensor(
-        out=half_sin[:], in0=cos_half_less_1[:], scalar=1.0, in1=sin_half[:], op0=ALU.add, op1=ALU.mult
-    )
-    nc.vector.tensor_scalar_add(out=table[:, :, 0, :, 0], in0=cos_less_1[:], scalar1=1.0)
-    nc.vector.tensor_scalar_add(out=table[:, :, 1, :, 1], in0=cos_less_1[:], scalar1=1.0)
-    nc.vector.tensor_scalar_mul(out=table[:, :, 0, :, 1], in0=half_sin[:], scalar1=2.0)
-    nc.vector.tensor_scalar_mul(out=table[:, :, 1, :, 0], in0=half_sin[:], scalar1=-2.0)
-    return table
+
+    def from_quarter(sin_quarter):
+        nc.vector.scalar_tensor_tensor(
+            out=cos_half_less_1[:], in0=sin_quarter[:], scalar=-2.0, in1=sin_quarter[:], op0=ALU.mult, op1=ALU.mult
+        )
+
+    def from_half(sin_half):
+        nc.vector.scalar_tensor_tensor(
+            out=cos_less_1[:], in0=sin_half[:], scalar=-2.0, in1=sin_half[:], op0=ALU.mult, op1=ALU.mult
+        )
+        nc.vector.scalar_tensor_tensor(
+            out=half_sin[:], in0=cos_half_less_1[:], scalar=1.0, in1=sin_half[:], op0=ALU.add, op1=ALU.mult
+        )
+
+    def write(which):
+        if which == 0:
+            nc.vector.tensor_scalar_add(out=table[:, :, 0, :, 0], in0=cos_less_1[:], scalar1=1.0)
+        elif which == 1:
+            nc.vector.tensor_scalar_add(out=table[:, :, 1, :, 1], in0=cos_less_1[:], scalar1=1.0)
+        elif which == 2:
+            nc.vector.tensor_scalar_mul(out=table[:, :, 0, :, 1], in0=half_sin[:], scalar1=2.0)
+        else:
+            nc.vector.tensor_scalar_mul(out=table[:, :, 1, :, 0], in0=half_sin[:], scalar1=-2.0)
+
+    return table, from_quarter, from_half, write
 
 
 def load_scale_planes(nc, planes, scales, first, width):
@@ -210,6 +205,14 @@ def tile_multiheadselfattention_pa_kernel(
 
         identity = keep.tile([P, P], F32, name="identity")
         make_identity(nc, identity[:])
+        position = keep.tile([P, POS_TILES], F32, name="position")
+        nc.gpsimd.iota(
+            position[:],
+            pattern=[[1, POS_TILES]],
+            base=0,
+            channel_multiplier=POS_TILES,
+            allow_small_or_imprecise_dtypes=True,
+        )
 
         idle_bank = psum.tile([P, P], F32, name="idle_bank", tag="bank")
 
@@ -219,10 +222,12 @@ def tile_multiheadselfattention_pa_kernel(
         for count in range(FIRST_IDLE_MATMULS):
             idle_matmul()
 
-        reduced = build_reduced_angles(nc, keep)
-
+        minus_fraction = build_turn_fractions(nc, keep, position)
+        sin_quarter = take_sine(nc, keep, minus_fraction, 4.0, "sin_quarter")
+        sin_half = take_sine(nc, keep, minus_fraction, 2.0, "sin_half")
         nc.vector.memset(plane_tiles[0][:, N_TILE:columns_of_a_weight].bitcast(I32), 0)
         nc.vector.memset(plane_tiles[1][:].bitcast(I32), 0)
+
         load_scale_planes(nc, plane_tiles[0], Wq_scales, N_TILE, N_TILE)
         load_words(1, 0)
         load_scale_planes(nc, plane_tiles[0], Wq_scales, 2 * N_TILE, columns_of_a_weight - 2 * N_TILE)
@@ -272,14 +277,15 @@ def tile_multiheadselfattention_pa_kernel(
             terms = products.tile([P, POS_TILES, 2, TILE_HEADS, HALF, 2], F32, name="terms")
             step_tiles[step] = (rotated, terms)
 
-        def project_piece(step, j, bank, piece):
+        def project_piece(step, j, bank, piece, alone=False):
             w = step // COL_TILES
             first = (step % COL_TILES) * N_TILE
             words_tile, offset, width = word_tiles[step][piece]
+            place = 0 if alone else offset
             for g in range(PASSES):
                 positions = slice(g * P, (g + 1) * P)
                 nc.tensor.matmul_mx(
-                    out=bank[:, offset : offset + width],
+                    out=bank[:, place : place + width],
                     lhsT=x_codes[j][:, positions].bitcast(FP8X4),
                     lhsT_scale=x_planes[j][:, positions],
                     rhs=words_tile[:, g, :].bitcast(FP8X4),
@@ -336,25 +342,60 @@ def tile_multiheadselfattention_pa_kernel(
                     out=out_rows[:, heads, late * HEAD_DIM : (late + 1) * HEAD_DIM], in_=rotated_last[:, :, late, :]
                 )
 
+        table, table_from_quarter, table_from_half, table_write = rotation_table(nc, keep)
         transpose_x(0, True)
         transpose_x(1, True)
+        table_from_quarter(sin_quarter)
+        table_from_half(sin_half)
+        table_write(0)
         quantize_x(0)
+        table_write(1)
         quantize_x(1)
-        sin_half, sin_quarter = take_sines(nc, keep, reduced)
-        table = build_rotation_table(nc, keep, sin_half, sin_quarter)
+        table_write(2)
+        table_write(3)
         open_step(0)
-        bank_0 = psum.tile([P, N_TILE], F32, name="bank", tag="bank")
-        project_piece(0, 0, bank_0, 0)
+        piece_heads = TILE_HEADS // 2
+        piece_shape = [P, 2, piece_heads, HALF, 2]
+        piece_terms = []
+        for piece in range(2):
+            early = keep.tile([P, 2, 2, piece_heads, HALF, 2], F32, name="early%d" % piece)
+            piece_terms.append(early)
+
+        def project_early(j, piece):
+            bank = psum.tile([P, N_TILE], F32, name="bank", tag="bank")
+            project_piece(0, j, bank, piece, alone=True)
+            return bank
+
+        def rotate_early(j, piece, bank):
+            nc.vector.tensor_tensor(
+                out=piece_terms[piece][:, j],
+                in0=bank[:, 0 : piece_heads * HEAD_DIM]
+                .rearrange("p (h i v) -> p v h i", i=HALF, v=2)
+                .unsqueeze(4)
+                .to_broadcast(piece_shape),
+                in1=table[:, j].unsqueeze(2).to_broadcast(piece_shape),
+                op=ALU.mult,
+            )
+            if j == 0:
+                return
+            rotated = step_tiles[0][0]
+            nc.gpsimd.tensor_tensor(
+                out=rotated[:, piece * piece_heads : (piece + 1) * piece_heads, 0:2, :].rearrange("p h j d -> p j h d"),
+                in0=piece_terms[piece][:, :, 0].rearrange("p j h i e -> p j h (i e)"),
+                in1=piece_terms[piece][:, :, 1].rearrange("p j h i e -> p j h (i e)"),
+                op=ALU.add,
+            )
+
+        bank_0 = project_early(0, 0)
         transpose_x(2, False)
-        bank_1 = psum.tile([P, N_TILE], F32, name="bank", tag="bank")
-        project_piece(0, 1, bank_1, 0)
+        bank_1 = project_early(1, 0)
         transpose_x(3, False)
+        rotate_early(0, 0, bank_0)
+        rotate_early(1, 0, bank_1)
         quantize_x(2)
         quantize_x(3)
-        project_piece(0, 0, bank_0, 1)
-        rotate(0, 0, bank_0)
-        project_piece(0, 1, bank_1, 1)
-        rotate(0, 1, bank_1)
+        for j in range(2):
+            rotate_early(j, 1, project_early(j, 1))
         for j in range(2, POS_TILES):
             rotate(0, j, project(0, j))
         for step in range(1, steps):

@@ -100,6 +100,10 @@ def rotation_table(nc, pool):
     half_sin = pool.tile(shape, F32, name="half_sin")
     cos_less_1 = pool.tile(shape, F32, name="cos_less_1")
     table = pool.tile([P, POS_TILES, 2, HALF, 2], F32, name="table")
+    twice = [P, POS_TILES, HALF, 2]
+    signs = pool.tile([P, 2], F32, name="signs")
+    nc.vector.memset(signs[:, 0:1], 2.0)
+    nc.vector.memset(signs[:, 1:2], -2.0)
 
     def from_quarter(sin_quarter):
         nc.vector.scalar_tensor_tensor(
@@ -116,13 +120,16 @@ def rotation_table(nc, pool):
 
     def write(which):
         if which == 0:
-            nc.vector.tensor_scalar_add(out=table[:, :, 0, :, 0], in0=cos_less_1[:], scalar1=1.0)
-        elif which == 1:
-            nc.vector.tensor_scalar_add(out=table[:, :, 1, :, 1], in0=cos_less_1[:], scalar1=1.0)
-        elif which == 2:
-            nc.vector.tensor_scalar_mul(out=table[:, :, 0, :, 1], in0=half_sin[:], scalar1=2.0)
+            nc.vector.tensor_scalar_add(
+                out=table[:, :, 0, :, :], in0=cos_less_1[:].unsqueeze(3).to_broadcast(twice), scalar1=1.0
+            )
         else:
-            nc.vector.tensor_scalar_mul(out=table[:, :, 1, :, 0], in0=half_sin[:], scalar1=-2.0)
+            nc.vector.tensor_tensor(
+                out=table[:, :, 1, :, :],
+                in0=half_sin[:].unsqueeze(3).to_broadcast(twice),
+                in1=signs[:].unsqueeze(1).unsqueeze(1).to_broadcast(twice),
+                op=ALU.mult,
+            )
 
     return table, from_quarter, from_half, write
 
@@ -308,7 +315,7 @@ def tile_multiheadselfattention_pa_kernel(
             heads = slice(first_head, first_head + TILE_HEADS)
             nc.vector.tensor_tensor(
                 out=terms[:, j],
-                in0=bank[:].rearrange("p (h i v) -> p v h i", i=HALF, v=2).unsqueeze(4).to_broadcast(pair_shape),
+                in0=bank[:].rearrange("p (h i e) -> p h i e", i=HALF, e=2).unsqueeze(1).to_broadcast(pair_shape),
                 in1=table[:, j].unsqueeze(2).to_broadcast(pair_shape),
                 op=ALU.mult,
             )
@@ -317,9 +324,9 @@ def tile_multiheadselfattention_pa_kernel(
             if step < steps - 1 or j < GPSIMD_LAST_TILES:
                 both = slice(j - 1, j + 1)
                 nc.gpsimd.tensor_tensor(
-                    out=rotated[:, :, both, :].rearrange("p h j d -> p j h d"),
-                    in0=terms[:, both, 0].rearrange("p j h i e -> p j h (i e)"),
-                    in1=terms[:, both, 1].rearrange("p j h i e -> p j h (i e)"),
+                    out=rotated[:, :, both, :].rearrange("p h j (i e) -> p j h i e", e=2),
+                    in0=terms[:, both, 0],
+                    in1=terms[:, both, 1][:, :, :, :, ::-1],
                     op=ALU.add,
                 )
                 if step == steps - 1:
@@ -333,9 +340,9 @@ def tile_multiheadselfattention_pa_kernel(
             rotated_last = results.tile([P, TILE_HEADS, POS_TILES, HEAD_DIM], F32, name="rotated")
             for late in range(j - 1, j + 1):
                 nc.vector.tensor_tensor(
-                    out=rotated_last[:, :, late, :],
-                    in0=terms[:, late, 0].rearrange("p h i e -> p h (i e)"),
-                    in1=terms[:, late, 1].rearrange("p h i e -> p h (i e)"),
+                    out=rotated_last[:, :, late, :].rearrange("p h (i e) -> p h i e", e=2),
+                    in0=terms[:, late, 0],
+                    in1=terms[:, late, 1][:, :, :, ::-1],
                     op=ALU.add,
                 )
                 nc.sync.dma_start(
@@ -351,8 +358,6 @@ def tile_multiheadselfattention_pa_kernel(
         quantize_x(0)
         table_write(1)
         quantize_x(1)
-        table_write(2)
-        table_write(3)
         open_step(0)
         piece_heads = TILE_HEADS // 2
         piece_shape = [P, 2, piece_heads, HALF, 2]
@@ -370,8 +375,8 @@ def tile_multiheadselfattention_pa_kernel(
             nc.vector.tensor_tensor(
                 out=piece_terms[piece][:, j],
                 in0=bank[:, 0 : piece_heads * HEAD_DIM]
-                .rearrange("p (h i v) -> p v h i", i=HALF, v=2)
-                .unsqueeze(4)
+                .rearrange("p (h i e) -> p h i e", i=HALF, e=2)
+                .unsqueeze(1)
                 .to_broadcast(piece_shape),
                 in1=table[:, j].unsqueeze(2).to_broadcast(piece_shape),
                 op=ALU.mult,
@@ -380,9 +385,11 @@ def tile_multiheadselfattention_pa_kernel(
                 return
             rotated = step_tiles[0][0]
             nc.gpsimd.tensor_tensor(
-                out=rotated[:, piece * piece_heads : (piece + 1) * piece_heads, 0:2, :].rearrange("p h j d -> p j h d"),
-                in0=piece_terms[piece][:, :, 0].rearrange("p j h i e -> p j h (i e)"),
-                in1=piece_terms[piece][:, :, 1].rearrange("p j h i e -> p j h (i e)"),
+                out=rotated[:, piece * piece_heads : (piece + 1) * piece_heads, 0:2, :].rearrange(
+                    "p h j (i e) -> p j h i e", e=2
+                ),
+                in0=piece_terms[piece][:, :, 0],
+                in1=piece_terms[piece][:, :, 1][:, :, :, :, ::-1],
                 op=ALU.add,
             )
 

import math

import concourse.mybir as mybir
from concourse.masks import make_identity

F32 = mybir.dt.float32
BF16 = mybir.dt.bfloat16
I32 = mybir.dt.int32
U32 = mybir.dt.uint32
U8 = mybir.dt.uint8
FP8X4 = mybir.dt.float8_e4m3fn_x4
ALU = mybir.AluOpType
ACT = mybir.ActivationFunctionType

P = 128
SEQ = 512
EMB = 2048
HEADS = 16
HEAD_DIM = 128
HALF = HEAD_DIM // 2
RADIX = 4
DIGITS = 3
assert RADIX**DIGITS == HALF
ROPE_BASE = 10000.0

PACK = 4
K_PASS = P * PACK
PASSES = EMB // K_PASS
POS_TILES = SEQ // P
N_TILE = 512
TILE_HEADS = N_TILE // HEAD_DIM
COL_TILES = HEADS * HEAD_DIM // N_TILE
PLANE_ROWS = 4
QUADRANTS = 4
FIRST_IDLE_MATMULS = 3
GPSIMD_LAST_TILES = 2

TWO_PI = 2.0 * math.pi
ROUND_MAGIC = 1.5 * 2.0**23

FLOPS = 2 * SEQ * EMB * 2 * HEADS * HEAD_DIM


def build_turn_fractions(nc, pool, position):
    powers = pool.tile([P, DIGITS, RADIX], F32, name="powers")
    nc.vector.memset(powers[:], 1.0)
    for digit in range(DIGITS):
        for c in range(1, RADIX):
            nc.vector.tensor_scalar_mul(
                out=powers[:, digit, c : c + 1],
                in0=powers[:, digit, 0:1],
                scalar1=ROPE_BASE ** (-2.0 * c * RADIX**digit / HEAD_DIM),
            )

    square = [P, RADIX, RADIX]
    low = pool.tile(square, F32, name="low")
    nc.vector.tensor_tensor(
        out=low[:],
        in0=powers[:, 1, :].unsqueeze(2).to_broadcast(square),
        in1=powers[:, 0, :].unsqueeze(1).to_broadcast(square),
        op=ALU.mult,
    )
    high = pool.tile([P, POS_TILES, RADIX], F32, name="high")
    nc.vector.scalar_tensor_tensor(
        out=high[:],
        in0=position[:].unsqueeze(2).to_broadcast([P, POS_TILES, RADIX]),
        scalar=1.0 / TWO_PI,
        in1=powers[:, 2, :].unsqueeze(1).to_broadcast([P, POS_TILES, RADIX]),
        op0=ALU.mult,
        op1=ALU.mult,
    )
    shape = [P, POS_TILES, HALF]
    outer = [P, POS_TILES * RADIX, RADIX * RADIX]
    angle = pool.tile(shape, F32, name="angle")
    nc.vector.tensor_tensor(
        out=angle[:].rearrange("p j (a f) -> p (j a) f", a=RADIX),
        in0=high[:].rearrange("p j a -> p (j a)").unsqueeze(2).to_broadcast(outer),
        in1=low[:].rearrange("p b c -> p (b c)").unsqueeze(1).to_broadcast(outer),
        op=ALU.mult,
    )

    shifted = pool.tile(shape, F32, name="shifted")
    minus_fraction = pool.tile(shape, F32, name="minus_fraction")
    nc.vector.tensor_scalar_add(out=shifted[:], in0=angle[:], scalar1=ROUND_MAGIC)
    nc.vector.scalar_tensor_tensor(
        out=minus_fraction[:], in0=shifted[:], scalar=ROUND_MAGIC, in1=angle[:], op0=ALU.subtract, op1=ALU.subtract
    )
    return minus_fraction


def take_sine(nc, pool, minus_fraction, part, name):
    sine = pool.tile([P, POS_TILES, HALF], F32, name=name)
    nc.scalar.activation(out=sine[:], in_=minus_fraction[:], func=ACT.Sin, scale=-TWO_PI / part)
    return sine


def rotation_table(nc, pool):
    shape = [P, POS_TILES, HALF]
    cos_half_less_1 = pool.tile(shape, F32, name="cos_half_less_1")
    half_sin = pool.tile(shape, F32, name="half_sin")
    cos_less_1 = pool.tile(shape, F32, name="cos_less_1")
    table = pool.tile([P, POS_TILES, 2, HALF, 2], F32, name="table")
    twice = [P, POS_TILES, HALF, 2]
    signs = pool.tile([P, 2], F32, name="signs")
    nc.vector.memset(signs[:, 0:1], 2.0)
    nc.vector.memset(signs[:, 1:2], -2.0)

    def from_quarter(sin_quarter):
        nc.vector.scalar_tensor_tensor(
            out=cos_half_less_1[:], in0=sin_quarter[:], scalar=-2.0, in1=sin_quarter[:], op0=ALU.mult, op1=ALU.mult
        )

    def from_half(sin_half):
        nc.vector.scalar_tensor_tensor(
            out=cos_less_1[:], in0=sin_half[:], scalar=-2.0, in1=sin_half[:], op0=ALU.mult, op1=ALU.mult
        )
        nc.vector.scalar_tensor_tensor(
            out=half_sin[:], in0=cos_half_less_1[:], scalar=1.0, in1=sin_half[:], op0=ALU.add, op1=ALU.mult
        )

    def write(which):
        if which == 0:
            nc.vector.tensor_scalar_add(
                out=table[:, :, 0, :, :], in0=cos_less_1[:].unsqueeze(3).to_broadcast(twice), scalar1=1.0
            )
        else:
            nc.vector.tensor_tensor(
                out=table[:, :, 1, :, :],
                in0=half_sin[:].unsqueeze(3).to_broadcast(twice),
                in1=signs[:].unsqueeze(1).unsqueeze(1).to_broadcast(twice),
                op=ALU.mult,
            )

    return table, from_quarter, from_half, write


def load_scale_planes(nc, planes, scales, first, width):
    for quadrant in range(QUADRANTS):
        row = 32 * quadrant
        nc.sync.dma_start(
            out=planes[row : row + PASSES * PLANE_ROWS, first : first + width].bitcast(I32),
            in_=scales[:, PLANE_ROWS * quadrant : PLANE_ROWS * (quadrant + 1), first : first + width].bitcast(I32),
        )


def load_weight_columns(nc, words_tile, words, first, width):
    nc.sync.dma_start(
        out=words_tile[:].bitcast(I32),
        in_=words[:, :, first : first + width, :].rearrange("g p n t -> p g (n t)").bitcast(I32),
    )


def column_pieces(step):
    if step == 0:
        return [N_TILE // 2, N_TILE // 2]
    return [N_TILE]


def tile_multiheadselfattention_pa_kernel(
    tc, x, Wq_words, Wq_scales, Wk_words, Wk_scales, out_0, out_1
):
    nc = tc.nc
    weights = [(Wq_words, Wq_scales, out_0), (Wk_words, Wk_scales, out_1)]
    steps = len(weights) * COL_TILES
    columns_of_a_weight = HEADS * HEAD_DIM

    with tc.manual_schedule(), tc.tile_pool(name="keep", bufs=1) as keep, tc.tile_pool(
        name="products", bufs=3
    ) as products, tc.tile_pool(name="results", bufs=3) as results, tc.psum_pool(name="psum", bufs=8) as psum:
        x_rows = x.rearrange("b (m j) k -> m (b j) k", j=POS_TILES)
        x_tiles = []
        for j in range(POS_TILES):
            x_tile = keep.tile([P, EMB], BF16, name="x%d" % j)
            x_tiles.append(x_tile)
        plane_tiles = []
        for w in range(len(weights)):
            planes = keep.tile([P, columns_of_a_weight], U8, name="planes%d" % w, align_bytes=256)
            plane_tiles.append(planes)
        word_tiles = []
        for step in range(steps):
            piece_tiles = []
            offset = 0
            for width in column_pieces(step):
                words_tile = keep.tile([P, PASSES, width], U32, name="w%d_%d" % (step, offset), align_bytes=256)
                piece_tiles.append((words_tile, offset, width))
                offset += width
            word_tiles.append(piece_tiles)

        def load_x(j, pieces):
            width = EMB // pieces
            for first in range(0, EMB, width):
                nc.sync.dma_start(out=x_tiles[j][:, first : first + width], in_=x_rows[:, j, first : first + width])

        def load_words(step, piece):
            words_tile, offset, width = word_tiles[step][piece]
            load_weight_columns(
                nc, words_tile, weights[step // COL_TILES][0], (step % COL_TILES) * N_TILE + offset, width
            )

        load_x(0, 2)
        load_x(1, 1)
        zero = keep.tile([P, 1], F32, name="zero")
        warm = keep.tile([P, 1], F32, name="warm")
        nc.vector.memset(zero[:], 0.0)
        nc.scalar.activation(out=warm[:], in_=zero[:], func=ACT.Sin)
        nc.vector.memset(plane_tiles[0][:, 0:N_TILE].bitcast(I32), 0)
        load_scale_planes(nc, plane_tiles[0], Wq_scales, 0, N_TILE)
        load_words(0, 0)
        load_x(2, 1)
        load_x(3, 1)
        load_words(0, 1)

        identity = keep.tile([P, P], F32, name="identity")
        make_identity(nc, identity[:])
        position = keep.tile([P, POS_TILES], F32, name="position")
        nc.gpsimd.iota(
            position[:],
            pattern=[[1, POS_TILES]],
            base=0,
            channel_multiplier=POS_TILES,
            allow_small_or_imprecise_dtypes=True,
        )

        idle_bank = psum.tile([P, P], F32, name="idle_bank", tag="bank")

        def idle_matmul():
            nc.tensor.matmul(out=idle_bank[:], lhsT=identity[:], rhs=identity[:], start=True, stop=True)

        for count in range(FIRST_IDLE_MATMULS):
            idle_matmul()

        minus_fraction = build_turn_fractions(nc, keep, position)
        sin_quarter = take_sine(nc, keep, minus_fraction, 4.0, "sin_quarter")
        sin_half = take_sine(nc, keep, minus_fraction, 2.0, "sin_half")
        nc.vector.memset(plane_tiles[0][:, N_TILE:columns_of_a_weight].bitcast(I32), 0)
        nc.vector.memset(plane_tiles[1][:].bitcast(I32), 0)

        load_scale_planes(nc, plane_tiles[0], Wq_scales, N_TILE, N_TILE)
        load_words(1, 0)
        load_scale_planes(nc, plane_tiles[0], Wq_scales, 2 * N_TILE, columns_of_a_weight - 2 * N_TILE)
        for step in range(2, COL_TILES):
            load_words(step, 0)
        load_scale_planes(nc, plane_tiles[1], Wk_scales, 0, columns_of_a_weight)
        for step in range(COL_TILES, steps):
            load_words(step, 0)

        grouped_tiles = {}
        x_codes = {}
        x_planes = {}

        def transpose_x(j, idle_matmuls):
            pair_words = x_tiles[j][:].bitcast(F32)
            grouped = keep.tile([P, PASSES * P * PACK], BF16, name="grouped%d" % j, align_bytes=64)
            grouped_words = grouped[:].bitcast(F32).rearrange("p (g m u) -> p g m u", g=PASSES, u=2)
            for first_pass in range(0, PASSES, 2):
                flipped = psum.tile([P, 2, 2, P], F32, name="flipped", tag="bank")
                for g in range(first_pass, first_pass + 2):
                    for u in range(2):
                        nc.tensor.transpose(
                            out=flipped[:, g - first_pass, u, :],
                            in_=pair_words[:, 2 * P * g + u : 2 * P * (g + 1) : 2],
                            identity=identity[:],
                        )
                if idle_matmuls:
                    idle_matmul()
                nc.scalar.copy(
                    out=grouped_words[:, first_pass : first_pass + 2, :, :],
                    in_=flipped[:].rearrange("p g u m -> p g m u"),
                )
            grouped_tiles[j] = grouped

        def quantize_x(j):
            codes = keep.tile([P, PASSES * P], U32, name="x_codes%d" % j, align_bytes=256)
            plane = keep.tile([P, PASSES * P], U8, name="x_plane%d" % j, align_bytes=256)
            nc.vector.quantize_mx(out=codes[:].bitcast(FP8X4), scales=plane[:], in_=grouped_tiles[j][:])
            x_codes[j] = codes
            x_planes[j] = plane

        pair_shape = [P, 2, TILE_HEADS, HALF, 2]
        step_tiles = {}

        def open_step(step):
            rotated = results.tile([P, TILE_HEADS, POS_TILES, HEAD_DIM], F32, name="rotated")
            terms = products.tile([P, POS_TILES, 2, TILE_HEADS, HALF, 2], F32, name="terms")
            step_tiles[step] = (rotated, terms)

        def project_piece(step, j, bank, piece, alone=False):
            w = step // COL_TILES
            first = (step % COL_TILES) * N_TILE
            words_tile, offset, width = word_tiles[step][piece]
            place = 0 if alone else offset
            for g in range(PASSES):
                positions = slice(g * P, (g + 1) * P)
                nc.tensor.matmul_mx(
                    out=bank[:, place : place + width],
                    lhsT=x_codes[j][:, positions].bitcast(FP8X4),
                    lhsT_scale=x_planes[j][:, positions],
                    rhs=words_tile[:, g, :].bitcast(FP8X4),
                    rhs_scale=plane_tiles[w][PLANE_ROWS * g : P, first + offset : first + offset + width],
                    start=(g == 0),
                    stop=(g == PASSES - 1),
                )

        def project(step, j):
            bank = psum.tile([P, N_TILE], F32, name="bank", tag="bank")
            for piece in range(len(word_tiles[step])):
                project_piece(step, j, bank, piece)
            return bank

        def rotate(step, j, bank):
            rotated, terms = step_tiles[step]
            out = weights[step // COL_TILES][2]
            out_rows = out.rearrange("b h (m j) d -> m (b h) (j d)", j=POS_TILES)
            first_head = (step % COL_TILES) * TILE_HEADS
            heads = slice(first_head, first_head + TILE_HEADS)
            nc.vector.tensor_tensor(
                out=terms[:, j],
                in0=bank[:].rearrange("p (h i e) -> p h i e", i=HALF, e=2).unsqueeze(1).to_broadcast(pair_shape),
                in1=table[:, j].unsqueeze(2).to_broadcast(pair_shape),
                op=ALU.mult,
            )
            if j % 2 == 0:
                return
            if step < steps - 1 or j < GPSIMD_LAST_TILES:
                both = slice(j - 1, j + 1)
                nc.gpsimd.tensor_tensor(
                    out=rotated[:, :, both, :].rearrange("p h j (i e) -> p j h i e", e=2),
                    in0=terms[:, both, 0],
                    in1=terms[:, both, 1][:, :, :, :, ::-1],
                    op=ALU.add,
                )
                if step == steps - 1:
                    nc.scalar.dma_start(
                        out=out_rows[:, heads, 0 : GPSIMD_LAST_TILES * HEAD_DIM],
                        in_=rotated[:, :, 0:GPSIMD_LAST_TILES, :].rearrange("m h j d -> m h (j d)"),
                    )
                elif j == POS_TILES - 1:
                    nc.scalar.dma_start(out=out_rows[:, heads, :], in_=rotated[:].rearrange("m h j d -> m h (j d)"))
                return
            rotated_last = results.tile([P, TILE_HEADS, POS_TILES, HEAD_DIM], F32, name="rotated")
            for late in range(j - 1, j + 1):
                nc.vector.tensor_tensor(
                    out=rotated_last[:, :, late, :].rearrange("p h (i e) -> p h i e", e=2),
                    in0=terms[:, late, 0],
                    in1=terms[:, late, 1][:, :, :, ::-1],
                    op=ALU.add,
                )
                nc.sync.dma_start(
                    out=out_rows[:, heads, late * HEAD_DIM : (late + 1) * HEAD_DIM], in_=rotated_last[:, :, late, :]
                )

        table, table_from_quarter, table_from_half, table_write = rotation_table(nc, keep)
        transpose_x(0, True)
        transpose_x(1, True)
        table_from_quarter(sin_quarter)
        table_from_half(sin_half)
        table_write(0)
        quantize_x(0)
        table_write(1)
        quantize_x(1)
        open_step(0)
        piece_heads = TILE_HEADS // 2
        piece_shape = [P, 2, piece_heads, HALF, 2]
        piece_terms = []
        for piece in range(2):
            early = keep.tile([P, 2, 2, piece_heads, HALF, 2], F32, name="early%d" % piece)
            piece_terms.append(early)

        def project_early(j, piece):
            bank = psum.tile([P, N_TILE], F32, name="bank", tag="bank")
            project_piece(0, j, bank, piece, alone=True)
            return bank

        def rotate_early(j, piece, bank):
            nc.vector.tensor_tensor(
                out=piece_terms[piece][:, j],
                in0=bank[:, 0 : piece_heads * HEAD_DIM]
                .rearrange("p (h i e) -> p h i e", i=HALF, e=2)
                .unsqueeze(1)
                .to_broadcast(piece_shape),
                in1=table[:, j].unsqueeze(2).to_broadcast(piece_shape),
                op=ALU.mult,
            )
            if j == 0:
                return
            rotated = step_tiles[0][0]
            nc.gpsimd.tensor_tensor(
                out=rotated[:, piece * piece_heads : (piece + 1) * piece_heads, 0:2, :].rearrange(
                    "p h j (i e) -> p j h i e", e=2
                ),
                in0=piece_terms[piece][:, :, 0],
                in1=piece_terms[piece][:, :, 1][:, :, :, :, ::-1],
                op=ALU.add,
            )

        bank_0 = project_early(0, 0)
        transpose_x(2, False)
        bank_1 = project_early(1, 0)
        transpose_x(3, False)
        rotate_early(0, 0, bank_0)
        rotate_early(1, 0, bank_1)
        quantize_x(2)
        quantize_x(3)
        for j in range(2):
            rotate_early(j, 1, project_early(j, 1))
        for j in range(2, POS_TILES):
            rotate(0, j, project(0, j))
        for step in range(1, steps):
            open_step(step)
            for j in range(POS_TILES):
                rotate(step, j, project(step, j))
